import numpy as np
import ml_dtypes


def mxq(x, axis, fmt="e4m3"):
    dtype, down = {"e4m3": (ml_dtypes.float8_e4m3fn, 7), "e5m2": (ml_dtypes.float8_e5m2, 14)}[fmt]
    v = np.moveaxis(np.asarray(x, np.float32).astype(ml_dtypes.bfloat16).astype(np.float64), axis, -1)
    blocks = v.reshape(v.shape[:-1] + (-1, 32))
    amax = np.abs(blocks).max(-1, keepdims=True)
    byte = np.maximum(np.where(amax > 0, np.frexp(amax)[1] - 1 + 127, 0) - down, 1)
    scale = np.exp2(byte - 127.0)
    codes = (blocks / scale).astype(np.float32).astype(dtype).astype(np.float64)
    return np.moveaxis((codes * scale).reshape(v.shape), -1, axis)


WIDE = False


def mx_kscale(k):
    if not WIDE:
        return np.ones(k)
    levels = np.array([10, -10, 5, -5, 0])
    a = np.random.permutation(np.resize(levels, k // 512 * 4)).reshape(k // 512, 4)
    idx = np.arange(k)
    return np.exp2(a[idx // 512, idx % 128 // 32])


BF16 = ml_dtypes.bfloat16


def bf(x):
    return np.asarray(x, np.float32).astype(BF16)


def f64(x):
    return np.asarray(x).astype(np.float64)


E2M1 = np.array([0.0, 0.5, 1.0, 1.5, 2.0, 3.0, 4.0, 6.0, -0.0, -0.5, -1.0, -1.5, -2.0, -3.0, -4.0, -6.0])


def pack_weight(w, fmt):
    k, n = w.shape
    w = f64(bf(w)).reshape(k // 32, 32, n)
    amax = np.abs(w).max(1)
    if fmt == "e4m3":
        byte = np.frexp(amax)[1] - 1 + 127 - 7
    else:
        mant, ex = np.frexp(amax / 6.0)
        byte = np.where(mant > 0.5, ex, ex - 1) + 127
    byte = np.clip(np.where(amax > 0, byte, 1), 1, 254)
    scaled = (w * np.exp2(127.0 - byte)[:, None, :]).reshape(k, n).astype(np.float32)
    by_word = np.ascontiguousarray(scaled.reshape(k // 512, 128, 4, n).transpose(0, 1, 3, 2))
    if fmt == "e4m3":
        words = by_word.astype(ml_dtypes.float8_e4m3fn).view(np.uint8)
    else:
        c = by_word.astype(ml_dtypes.float4_e2m1fn).view(np.uint8) & 0xF
        words = c[..., 0::2] | (c[..., 1::2] << 4)
    return np.ascontiguousarray(words), np.ascontiguousarray(byte.astype(np.uint8).reshape(k // 512, 16, n))


def unpack_weight(words, scales, fmt):
    g, p, n, _ = words.shape
    if fmt == "e4m3":
        vals = np.ascontiguousarray(words).view(ml_dtypes.float8_e4m3fn).astype(np.float64)
    else:
        nib = np.empty((g, p, n, 4), np.uint8)
        nib[..., 0::2] = words & 0xF
        nib[..., 1::2] = words >> 4
        vals = E2M1[nib]
    vals = vals * np.repeat(np.exp2(scales.astype(np.float64) - 127.0), 8, axis=1)[..., None]
    return vals.transpose(0, 1, 3, 2).reshape(g * 512, n)


B, N, SIZE, CH = 4096, 16, 512, 256


def sigmoid(v):
    return 1.0 / (1.0 + np.exp(-v))


def setup_inputs():
    s = mx_kscale(SIZE)
    d = {"z0": bf(np.random.standard_normal((B, SIZE)) * s),
         "h_tilde": bf(np.random.standard_normal((B, CH)) * np.sqrt(N)),
         "fc_sum": bf(np.random.standard_normal((B, CH)) * 1.2)}
    for g in ("i", "o", "u"):
        words, scales = pack_weight((np.random.standard_normal((CH, SIZE)) / np.sqrt(SIZE) / s).T, "e4m3")
        d["W_" + g + "_words"] = words
        d["W_" + g + "_scales"] = scales
        d["U_" + g] = bf(np.random.standard_normal((CH, CH)) / np.sqrt(CH * N))
        d["b_" + g] = bf(np.random.standard_normal(CH) * 0.5)
    return d


def reference(z0, h_tilde, fc_sum, W_i_words, W_i_scales, U_i, b_i, W_o_words, W_o_scales, U_o, b_o, W_u_words, W_u_scales, U_u, b_u):
    zq = mxq(f64(z0), 1, "e4m3")
    ht = f64(h_tilde)
    i_j = sigmoid((zq @ unpack_weight(W_i_words, W_i_scales, "e4m3")) + ht @ f64(U_i).T + f64(b_i))
    o_j = sigmoid((zq @ unpack_weight(W_o_words, W_o_scales, "e4m3")) + ht @ f64(U_o).T + f64(b_o))
    u_j = np.tanh((zq @ unpack_weight(W_u_words, W_u_scales, "e4m3")) + ht @ f64(U_u).T + f64(b_u))
    c_j = i_j * u_j + f64(fc_sum)
    h_j = o_j * np.tanh(c_j)
    return np.concatenate([h_j, c_j], axis=-1)

@@ -1,0 +1,215 @@
+from contextlib import ExitStack
+
+import concourse.mybir as mybir
+from concourse.masks import make_identity
+
+F32 = mybir.dt.float32
+BF16 = mybir.dt.bfloat16
+I32 = mybir.dt.int32
+U32 = mybir.dt.uint32
+U8 = mybir.dt.uint8
+FP8X4 = mybir.dt.float8_e4m3fn_x4
+ACT = mybir.ActivationFunctionType
+ALU = mybir.AluOpType
+
+P = 128
+NODES = 4096
+FEAT = 512
+CH = 256
+K_CHUNKS = CH // P
+TILES = NODES // P
+PAIR = 2
+PAIRS = TILES // PAIR
+CHUNK = 4
+GATES = 3
+
+FLOPS = 2 * NODES * GATES * CH * (FEAT + CH)
+
+
+def tile_treelstm_pb_t_kernel(
+    tc,
+    z0,
+    h_tilde,
+    fc_sum,
+    W_i_words,
+    W_i_scales,
+    U_i,
+    b_i,
+    W_o_words,
+    W_o_scales,
+    U_o,
+    b_o,
+    W_u_words,
+    W_u_scales,
+    U_u,
+    b_u,
+    out,
+):
+    nc = tc.nc
+    gate_words = [W_i_words, W_u_words, W_o_words]
+    gate_scales = [W_i_scales, W_u_scales, W_o_scales]
+    gate_u = [U_i, U_u, U_o]
+    gate_b = [b_i, b_u, b_o]
+    gate_func = [ACT.Sigmoid, ACT.Tanh, ACT.Sigmoid]
+
+    z_view = z0.rearrange("(p t) k -> p t k", t=TILES)
+    h_view = h_tilde.rearrange("(p t) k -> p t k", t=TILES)
+    fc_view = fc_sum.rearrange("(p t) c -> p t c", t=TILES)
+    out_view = out.rearrange("(p t) c -> p t c", t=TILES)
+
+    with ExitStack() as ctx:
+        consts = ctx.enter_context(tc.tile_pool(name="consts", bufs=1))
+        inputs = ctx.enter_context(tc.tile_pool(name="inputs", bufs=1))
+        work = ctx.enter_context(tc.tile_pool(name="work", bufs=3))
+        results = ctx.enter_context(tc.tile_pool(name="results", bufs=6))
+        psum_tr = ctx.enter_context(tc.psum_pool(name="psum_tr", bufs=1))
+        psum_prod = ctx.enter_context(tc.psum_pool(name="psum_prod", bufs=3))
+
+        w_planes = consts.tile([P, GATES * CH], U8, align_bytes=64)
+        nc.vector.memset(w_planes[:].bitcast(I32), 0)
+
+        ident_f32 = consts.tile([P, P], F32)
+        make_identity(nc, ident_f32[:])
+        ident_bf16 = consts.tile([P, P], BF16)
+        make_identity(nc, ident_bf16[:])
+
+        z_sb = []
+        h_sb = []
+        fc_sb = []
+        for c in range(TILES // CHUNK):
+            z_sb.append(inputs.tile([P, CHUNK, FEAT], BF16, name="z_sb%d" % c))
+            h_sb.append(inputs.tile([P, CHUNK, CH], BF16, name="h_sb%d" % c))
+            fc_sb.append(inputs.tile([P, CHUNK, CH], BF16, name="fc_sb%d" % c))
+
+        def load_chunk(c):
+            tiles = slice(c * CHUNK, (c + 1) * CHUNK)
+            nc.sync.dma_start(out=z_sb[c][:], in_=z_view[:, tiles, :])
+            nc.sync.dma_start(out=h_sb[c][:], in_=h_view[:, tiles, :])
+            nc.sync.dma_start(out=fc_sb[c][:], in_=fc_view[:, tiles, :])
+
+        load_chunk(0)
+
+        u_rows = consts.tile([P, GATES, K_CHUNKS, CH], BF16)
+        for g in range(GATES):
+            nc.sync.dma_start(out=u_rows[:, g, :, :], in_=gate_u[g].rearrange("(half p) k -> p half k", p=P))
+
+        for g in range(GATES):
+            rows = gate_scales[g].rearrange("o q n -> (o q) n")
+            for quad in range(4):
+                nc.sync.dma_start(
+                    out=w_planes[32 * quad : 32 * quad + 4, g * CH : (g + 1) * CH].bitcast(I32),
+                    in_=rows[4 * quad : 4 * quad + 4, :].bitcast(I32),
+                )
+
+        w_codes = consts.tile([P, GATES, 4 * CH], U8, align_bytes=64)
+        for g in range(GATES):
+            nc.sync.dma_start(
+                out=w_codes[:, g, :].bitcast(I32),
+                in_=gate_words[g].rearrange("o p n t -> (o p) (n t)").bitcast(I32),
+            )
+
+        bias = consts.tile([P, GATES, CH], BF16)
+        for g in range(GATES):
+            nc.scalar.dma_start(out=bias[:, g, :], in_=gate_b[g].partition_broadcast(P))
+
+        for c in range(1, TILES // CHUNK):
+            load_chunk(c)
+
+        uT = consts.tile([P, K_CHUNKS, GATES * CH], BF16)
+        for g in range(GATES):
+            uT_ps = psum_tr.tile([P, K_CHUNKS, K_CHUNKS, P], BF16, tag="hT_ps")
+            for kc in range(K_CHUNKS):
+                for half in range(K_CHUNKS):
+                    nc.tensor.transpose(
+                        uT_ps[:, kc, half, :], u_rows[:, g, half, kc * P : (kc + 1) * P], ident_bf16[:]
+                    )
+            nc.scalar.copy(
+                out=uT[:, :, g * CH : (g + 1) * CH], in_=uT_ps[:].rearrange("p kc half n -> p kc (half n)")
+            )
+
+        def prepare(j):
+            c = (j * PAIR) // CHUNK
+            first = (j * PAIR) % CHUNK
+
+            zT_ps = psum_tr.tile([P, PAIR, 2, P], F32, tag="zT_ps")
+            for a in range(PAIR):
+                words = z_sb[c][:, first + a, :].bitcast(F32)
+                for u in range(2):
+                    nc.tensor.transpose(zT_ps[:, a, u, :], words[:, u : FEAT // 2 : 2], ident_f32[:])
+            hT_ps = psum_tr.tile([P, PAIR, K_CHUNKS, P], BF16, tag="hT_ps")
+            for a in range(PAIR):
+                for kc in range(K_CHUNKS):
+                    nc.tensor.transpose(
+                        hT_ps[:, a, kc, :], h_sb[c][:, first + a, kc * P : (kc + 1) * P], ident_bf16[:]
+                    )
+
+            grouped = work.tile([P, PAIR * P * 4], BF16, align_bytes=64, tag="grouped")
+            nc.scalar.copy(
+                out=grouped[:].bitcast(F32).rearrange("p (a n u) -> p a n u", a=PAIR, u=2),
+                in_=zT_ps[:].rearrange("p a u n -> p a n u"),
+            )
+            hT = work.tile([P, PAIR, K_CHUNKS, P], BF16, tag="hT")
+            nc.scalar.copy(out=hT[:], in_=hT_ps[:])
+
+            z_codes = work.tile([P, PAIR * P], U32, align_bytes=64, tag="z_codes")
+            z_planes = work.tile([P, PAIR * P], U8, align_bytes=64, tag="z_planes")
+            nc.vector.quantize_mx(out=z_codes[:].bitcast(FP8X4), scales=z_planes[:], in_=grouped[:])
+            return z_codes, z_planes, hT
+
+        def compute(j, z_codes, z_planes, hT):
+            c = (j * PAIR) // CHUNK
+            first = (j * PAIR) % CHUNK
+            gates = []
+            for g in range(GATES):
+                channels = slice(g * CH, (g + 1) * CH)
+                plain_ps = psum_prod.tile([P, PAIR, CH], F32, tag="plain_ps")
+                for a in range(PAIR):
+                    for kc in range(K_CHUNKS):
+                        nc.tensor.matmul(
+                            plain_ps[:, a, :],
+                            lhsT=hT[:, a, kc, :],
+                            rhs=uT[:, kc, channels],
+                            start=(kc == 0),
+                            stop=(kc == K_CHUNKS - 1),
+                        )
+                mx_ps = psum_prod.tile([P, PAIR, CH], F32, tag="mx_ps")
+                for a in range(PAIR):
+                    nodes = slice(a * P, (a + 1) * P)
+                    nc.tensor.matmul_mx(
+                        out=mx_ps[:, a, :],
+                        lhsT=z_codes[:, nodes].bitcast(FP8X4),
+                        lhsT_scale=z_planes[:, nodes],
+                        rhs=w_codes[:, g, :].bitcast(FP8X4),
+                        rhs_scale=w_planes[:, channels],
+                        start=True,
+                        stop=True,
+                    )
+                pre = work.tile([P, PAIR, CH], F32, tag="pre")
+                nc.vector.tensor_tensor(
+                    out=pre[:],
+                    in0=plain_ps[:],
+                    in1=bias[:, g, :].unsqueeze(1).to_broadcast([P, PAIR, CH]),
+                    op=ALU.add,
+                )
+                nc.vector.tensor_tensor(out=pre[:], in0=mx_ps[:], in1=pre[:], op=ALU.add)
+                gate = work.tile([P, PAIR, CH], F32, tag="gate%d" % g)
+                nc.scalar.activation(out=gate[:], in_=pre[:], func=gate_func[g])
+                gates.append(gate)
+            gate_i, gate_uu, gate_o = gates
+
+            res = results.tile([P, PAIR, 2 * CH], F32, tag="res")
+            iu = work.tile([P, PAIR, CH], F32, tag="iu")
+            nc.gpsimd.tensor_tensor(out=iu[:], in0=gate_i[:], in1=gate_uu[:], op=ALU.mult)
+            nc.gpsimd.tensor_tensor(
+                out=res[:, :, CH:], in0=iu[:], in1=fc_sb[c][:, first : first + PAIR, :], op=ALU.add
+            )
+            tanh_c = work.tile([P, PAIR, CH], F32, tag="tanh_c")
+            nc.scalar.activation(out=tanh_c[:], in_=res[:, :, CH:], func=ACT.Tanh)
+            nc.gpsimd.tensor_tensor(out=res[:, :, :CH], in0=gate_o[:], in1=tanh_c[:], op=ALU.mult)
+            nc.sync.dma_start(out=out_view[:, j * PAIR : (j + 1) * PAIR, :], in_=res[:])
+
+        ready = prepare(0)
+        for j in range(PAIRS):
+            following = prepare(j + 1) if j + 1 < PAIRS else None
+            compute(j, *ready)
+            ready = following

@@ -127,89 +127,147 @@ def tile_treelstm_pb_t_kernel(
                 out=uT[:, :, g * CH : (g + 1) * CH], in_=uT_ps[:].rearrange("p kc half n -> p kc (half n)")
             )
 
-        def prepare(j):
-            c = (j * PAIR) // CHUNK
-            first = (j * PAIR) % CHUNK
+        zT_ps = {}
+        hT_ps = {}
+        grouped = {}
+        hT = {}
+        z_codes = {}
+        z_planes = {}
+        gates = {}
+        res = {}
+        tanh_c = {}
+        plain_ps = {}
+        mx_ps = {}
+        pre = {}
+        iu = {}
 
-            zT_ps = psum_tr.tile([P, PAIR, 2, P], F32, tag="zT_ps")
+        def chunk_rows(tiles_sb, j):
+            first = (j * PAIR) % CHUNK
+            return tiles_sb[(j * PAIR) // CHUNK][:, first : first + PAIR, :]
+
+        def transpose_pair(j):
+            zT_ps[j] = psum_tr.tile([P, PAIR, 2, P], F32, tag="zT_ps", name="zT_ps")
             for a in range(PAIR):
-                words = z_sb[c][:, first + a, :].bitcast(F32)
+                words = chunk_rows(z_sb, j)[:, a, :].bitcast(F32)
                 for u in range(2):
-                    nc.tensor.transpose(zT_ps[:, a, u, :], words[:, u : FEAT // 2 : 2], ident_f32[:])
-            hT_ps = psum_tr.tile([P, PAIR, K_CHUNKS, P], BF16, tag="hT_ps")
+                    nc.tensor.transpose(zT_ps[j][:, a, u, :], words[:, u : FEAT // 2 : 2], ident_f32[:])
+            hT_ps[j] = psum_tr.tile([P, PAIR, K_CHUNKS, P], BF16, tag="hT_ps", name="hT_ps")
             for a in range(PAIR):
                 for kc in range(K_CHUNKS):
                     nc.tensor.transpose(
-                        hT_ps[:, a, kc, :], h_sb[c][:, first + a, kc * P : (kc + 1) * P], ident_bf16[:]
+                        hT_ps[j][:, a, kc, :], chunk_rows(h_sb, j)[:, a, kc * P : (kc + 1) * P], ident_bf16[:]
                     )
 
-            grouped = work.tile([P, PAIR * P * 4], BF16, align_bytes=64, tag="grouped")
+        def copy_out(j):
+            grouped[j] = work.tile([P, PAIR * P * 4], BF16, align_bytes=64, tag="grouped", name="grouped")
             nc.scalar.copy(
-                out=grouped[:].bitcast(F32).rearrange("p (a n u) -> p a n u", a=PAIR, u=2),
-                in_=zT_ps[:].rearrange("p a u n -> p a n u"),
+                out=grouped[j][:].bitcast(F32).rearrange("p (a n u) -> p a n u", a=PAIR, u=2),
+                in_=zT_ps[j][:].rearrange("p a u n -> p a n u"),
             )
-            hT = work.tile([P, PAIR, K_CHUNKS, P], BF16, tag="hT")
-            nc.scalar.copy(out=hT[:], in_=hT_ps[:])
+            hT[j] = work.tile([P, PAIR, K_CHUNKS, P], BF16, tag="hT", name="hT")
+            nc.scalar.copy(out=hT[j][:], in_=hT_ps[j][:])
 
-            z_codes = work.tile([P, PAIR * P], U32, align_bytes=64, tag="z_codes")
-            z_planes = work.tile([P, PAIR * P], U8, align_bytes=64, tag="z_planes")
-            nc.vector.quantize_mx(out=z_codes[:].bitcast(FP8X4), scales=z_planes[:], in_=grouped[:])
-            return z_codes, z_planes, hT
+        def quantise(j):
+            z_codes[j] = work.tile([P, PAIR * P], U32, align_bytes=64, tag="z_codes", name="z_codes")
+            z_planes[j] = work.tile([P, PAIR * P], U8, align_bytes=64, tag="z_planes", name="z_planes")
+            nc.vector.quantize_mx(out=z_codes[j][:].bitcast(FP8X4), scales=z_planes[j][:], in_=grouped[j][:])
 
-        def compute(j, z_codes, z_planes, hT):
-            c = (j * PAIR) // CHUNK
-            first = (j * PAIR) % CHUNK
-            gates = []
-            for g in range(GATES):
-                channels = slice(g * CH, (g + 1) * CH)
-                plain_ps = psum_prod.tile([P, PAIR, CH], F32, tag="plain_ps")
-                for a in range(PAIR):
-                    for kc in range(K_CHUNKS):
-                        nc.tensor.matmul(
-                            plain_ps[:, a, :],
-                            lhsT=hT[:, a, kc, :],
-                            rhs=uT[:, kc, channels],
-                            start=(kc == 0),
-                            stop=(kc == K_CHUNKS - 1),
-                        )
-                mx_ps = psum_prod.tile([P, PAIR, CH], F32, tag="mx_ps")
-                for a in range(PAIR):
-                    nodes = slice(a * P, (a + 1) * P)
-                    nc.tensor.matmul_mx(
-                        out=mx_ps[:, a, :],
-                        lhsT=z_codes[:, nodes].bitcast(FP8X4),
-                        lhsT_scale=z_planes[:, nodes],
-                        rhs=w_codes[:, g, :].bitcast(FP8X4),
-                        rhs_scale=w_planes[:, channels],
-                        start=True,
-                        stop=True,
+        def plain_product(j, g):
+            bank = psum_prod.tile([P, PAIR, CH], F32, tag="plain_ps")
+            for a in range(PAIR):
+                for kc in range(K_CHUNKS):
+                    nc.tensor.matmul(
+                        bank[:, a, :],
+                        lhsT=hT[j][:, a, kc, :],
+                        rhs=uT[:, kc, g * CH : (g + 1) * CH],
+                        start=(kc == 0),
+                        stop=(kc == K_CHUNKS - 1),
                     )
-                pre = work.tile([P, PAIR, CH], F32, tag="pre")
-                nc.vector.tensor_tensor(
-                    out=pre[:],
-                    in0=plain_ps[:],
-                    in1=bias[:, g, :].unsqueeze(1).to_broadcast([P, PAIR, CH]),
-                    op=ALU.add,
+            return bank
+
+        def mx_product(j, g):
+            bank = psum_prod.tile([P, PAIR, CH], F32, tag="mx_ps")
+            for a in range(PAIR):
+                nodes = slice(a * P, (a + 1) * P)
+                nc.tensor.matmul_mx(
+                    out=bank[:, a, :],
+                    lhsT=z_codes[j][:, nodes].bitcast(FP8X4),
+                    lhsT_scale=z_planes[j][:, nodes],
+                    rhs=w_codes[:, g, :].bitcast(FP8X4),
+                    rhs_scale=w_planes[:, g * CH : (g + 1) * CH],
+                    start=True,
+                    stop=True,
                 )
-                nc.vector.tensor_tensor(out=pre[:], in0=mx_ps[:], in1=pre[:], op=ALU.add)
-                gate = work.tile([P, PAIR, CH], F32, tag="gate%d" % g)
-                nc.scalar.activation(out=gate[:], in_=pre[:], func=gate_func[g])
-                gates.append(gate)
-            gate_i, gate_uu, gate_o = gates
+            return bank
 
-            res = results.tile([P, PAIR, 2 * CH], F32, tag="res")
-            iu = work.tile([P, PAIR, CH], F32, tag="iu")
-            nc.gpsimd.tensor_tensor(out=iu[:], in0=gate_i[:], in1=gate_uu[:], op=ALU.mult)
-            nc.gpsimd.tensor_tensor(
-                out=res[:, :, CH:], in0=iu[:], in1=fc_sb[c][:, first : first + PAIR, :], op=ALU.add
+        def products(j, g):
+            if g == GATES - 1:
+                mx_ps[j, g] = mx_product(j, g)
+                plain_ps[j, g] = plain_product(j, g)
+            else:
+                plain_ps[j, g] = plain_product(j, g)
+                mx_ps[j, g] = mx_product(j, g)
+
+        def add_bias(j, g):
+            pre[j, g] = work.tile([P, PAIR, CH], F32, tag="pre", name="pre")
+            nc.vector.tensor_tensor(
+                out=pre[j, g][:],
+                in0=plain_ps[j, g][:],
+                in1=bias[:, g, :].unsqueeze(1).to_broadcast([P, PAIR, CH]),
+                op=ALU.add,
             )
-            tanh_c = work.tile([P, PAIR, CH], F32, tag="tanh_c")
-            nc.scalar.activation(out=tanh_c[:], in_=res[:, :, CH:], func=ACT.Tanh)
-            nc.gpsimd.tensor_tensor(out=res[:, :, :CH], in0=gate_o[:], in1=tanh_c[:], op=ALU.mult)
-            nc.sync.dma_start(out=out_view[:, j * PAIR : (j + 1) * PAIR, :], in_=res[:])
 
-        ready = prepare(0)
-        for j in range(PAIRS):
-            following = prepare(j + 1) if j + 1 < PAIRS else None
-            compute(j, *ready)
-            ready = following
+        def finish_gate(j, g):
+            nc.vector.tensor_tensor(out=pre[j, g][:], in0=mx_ps[j, g][:], in1=pre[j, g][:], op=ALU.add)
+            gates[j, g] = work.tile([P, PAIR, CH], F32, tag="gate%d" % g, name="gate%d" % g)
+            nc.scalar.activation(out=gates[j, g][:], in_=pre[j, g][:], func=gate_func[g])
+
+        def input_times_update(j):
+            iu[j] = work.tile([P, PAIR, CH], F32, tag="iu", name="iu")
+            nc.gpsimd.tensor_tensor(out=iu[j][:], in0=gates[j, 0][:], in1=gates[j, 1][:], op=ALU.mult)
+
+        def cell(j):
+            res[j] = results.tile([P, PAIR, 2 * CH], F32, tag="res", name="res")
+            nc.gpsimd.tensor_tensor(out=res[j][:, :, CH:], in0=iu[j][:], in1=chunk_rows(fc_sb, j), op=ALU.add)
+
+        def squash_cell(j):
+            tanh_c[j] = work.tile([P, PAIR, CH], F32, tag="tanh_c", name="tanh_c")
+            nc.scalar.activation(out=tanh_c[j][:], in_=res[j][:, :, CH:], func=ACT.Tanh)
+
+        def hidden(j):
+            nc.gpsimd.tensor_tensor(out=res[j][:, :, :CH], in0=gates[j, 2][:], in1=tanh_c[j][:], op=ALU.mult)
+            nc.sync.dma_start(out=out_view[:, j * PAIR : (j + 1) * PAIR, :], in_=res[j][:])
+
+        with tc.manual_schedule():
+            for j in range(2):
+                transpose_pair(j)
+                copy_out(j)
+            quantise(0)
+            products(0, 0)
+            add_bias(0, 0)
+            for j in range(PAIRS):
+                products(j, 1)
+                add_bias(j, 1)
+                finish_gate(j, 0)
+                if j + 1 < PAIRS:
+                    quantise(j + 1)
+
+                products(j, 2)
+                if j + 2 < PAIRS:
+                    transpose_pair(j + 2)
+                add_bias(j, 2)
+                finish_gate(j, 1)
+                input_times_update(j)
+                if j > 0:
+                    squash_cell(j - 1)
+                    hidden(j - 1)
+
+                if j + 2 < PAIRS:
+                    copy_out(j + 2)
+                if j + 1 < PAIRS:
+                    products(j + 1, 0)
+                    add_bias(j + 1, 0)
+                finish_gate(j, 2)
+                cell(j)
+            squash_cell(PAIRS - 1)
+            hidden(PAIRS - 1)

@@ -235,7 +235,7 @@ def tile_treelstm_pb_t_kernel(
             nc.scalar.activation(out=tanh_c[j][:], in_=res[j][:, :, CH:], func=ACT.Tanh)
 
         def hidden(j):
-            nc.gpsimd.tensor_tensor(out=res[j][:, :, :CH], in0=gates[j, 2][:], in1=tanh_c[j][:], op=ALU.mult)
+            nc.vector.tensor_tensor(out=res[j][:, :, :CH], in0=gates[j, 2][:], in1=tanh_c[j][:], op=ALU.mult)
             nc.sync.dma_start(out=out_view[:, j * PAIR : (j + 1) * PAIR, :], in_=res[j][:])
 
         with tc.manual_schedule():

@@ -16,12 +16,15 @@ P = 128
 NODES = 4096
 FEAT = 512
 CH = 256
-K_CHUNKS = CH // P
+HALVES = CH // P
 TILES = NODES // P
 PAIR = 2
 PAIRS = TILES // PAIR
-CHUNK = 4
+QUAD = 4
+QUADS = TILES // QUAD
 GATES = 3
+BLOCKS = GATES * HALVES
+AHEAD = 4
 
 FLOPS = 2 * NODES * GATES * CH * (FEAT + CH)
 
@@ -48,8 +51,8 @@ def tile_treelstm_pb_t_kernel(
     nc = tc.nc
     gate_words = [W_i_words, W_u_words, W_o_words]
     gate_scales = [W_i_scales, W_u_scales, W_o_scales]
-    gate_u = [U_i, U_u, U_o]
-    gate_b = [b_i, b_u, b_o]
+    gate_hidden_weight = [U_i, U_u, U_o]
+    gate_bias = [b_i, b_u, b_o]
     gate_func = [ACT.Sigmoid, ACT.Tanh, ACT.Sigmoid]
 
     z_view = z0.rearrange("(p t) k -> p t k", t=TILES)
@@ -60,13 +63,19 @@ def tile_treelstm_pb_t_kernel(
     with ExitStack() as ctx:
         consts = ctx.enter_context(tc.tile_pool(name="consts", bufs=1))
         inputs = ctx.enter_context(tc.tile_pool(name="inputs", bufs=1))
+        ahead = ctx.enter_context(tc.tile_pool(name="ahead", bufs=AHEAD + 2))
+        quads = ctx.enter_context(tc.tile_pool(name="quads", bufs=3))
+        blocks = ctx.enter_context(tc.tile_pool(name="blocks", bufs=2))
         work = ctx.enter_context(tc.tile_pool(name="work", bufs=3))
-        results = ctx.enter_context(tc.tile_pool(name="results", bufs=6))
+        results = ctx.enter_context(tc.tile_pool(name="results", bufs=4))
         psum_tr = ctx.enter_context(tc.psum_pool(name="psum_tr", bufs=1))
-        psum_prod = ctx.enter_context(tc.psum_pool(name="psum_prod", bufs=3))
+        psum_mx = ctx.enter_context(tc.psum_pool(name="psum_mx", bufs=2))
+        psum_gate = ctx.enter_context(tc.psum_pool(name="psum_gate", bufs=4))
 
         w_planes = consts.tile([P, GATES * CH], U8, align_bytes=64)
         nc.vector.memset(w_planes[:].bitcast(I32), 0)
+        bias_rows = consts.tile([P, P], BF16)
+        nc.vector.memset(bias_rows[:], 0.0)
 
         ident_f32 = consts.tile([P, P], F32)
         make_identity(nc, ident_f32[:])
@@ -76,56 +85,50 @@ def tile_treelstm_pb_t_kernel(
         z_sb = []
         h_sb = []
         fc_sb = []
-        for c in range(TILES // CHUNK):
-            z_sb.append(inputs.tile([P, CHUNK, FEAT], BF16, name="z_sb%d" % c))
-            h_sb.append(inputs.tile([P, CHUNK, CH], BF16, name="h_sb%d" % c))
-            fc_sb.append(inputs.tile([P, CHUNK, CH], BF16, name="fc_sb%d" % c))
+        for q in range(QUADS):
+            z_sb.append(inputs.tile([P, QUAD, FEAT], BF16, name="z_sb%d" % q))
+            h_sb.append(inputs.tile([P, QUAD, CH], BF16, name="h_sb%d" % q))
+            fc_sb.append(inputs.tile([P, QUAD, CH], BF16, name="fc_sb%d" % q))
 
-        def load_chunk(c):
-            tiles = slice(c * CHUNK, (c + 1) * CHUNK)
-            nc.sync.dma_start(out=z_sb[c][:], in_=z_view[:, tiles, :])
-            nc.sync.dma_start(out=h_sb[c][:], in_=h_view[:, tiles, :])
-            nc.sync.dma_start(out=fc_sb[c][:], in_=fc_view[:, tiles, :])
+        def load_operands(q):
+            nc.sync.dma_start(out=z_sb[q][:], in_=z_view[:, q * QUAD : (q + 1) * QUAD, :])
+            nc.sync.dma_start(out=h_sb[q][:], in_=h_view[:, q * QUAD : (q + 1) * QUAD, :])
 
-        load_chunk(0)
-
-        u_rows = consts.tile([P, GATES, K_CHUNKS, CH], BF16)
-        for g in range(GATES):
-            nc.sync.dma_start(out=u_rows[:, g, :, :], in_=gate_u[g].rearrange("(half p) k -> p half k", p=P))
+        def load_cells(q):
+            nc.sync.dma_start(out=fc_sb[q][:], in_=fc_view[:, q * QUAD : (q + 1) * QUAD, :])
 
         for g in range(GATES):
-            rows = gate_scales[g].rearrange("o q n -> (o q) n")
-            for quad in range(4):
-                nc.sync.dma_start(
-                    out=w_planes[32 * quad : 32 * quad + 4, g * CH : (g + 1) * CH].bitcast(I32),
-                    in_=rows[4 * quad : 4 * quad + 4, :].bitcast(I32),
-                )
+            nc.scalar.dma_start(
+                out=bias_rows[HALVES * g : HALVES * (g + 1), :],
+                in_=gate_bias[g].rearrange("(half c) -> half c", c=P),
+            )
+
+        load_operands(0)
+
+        u_rows = consts.tile([P, GATES, HALVES, CH], BF16)
+        for g in range(GATES):
+            nc.sync.dma_start(
+                out=u_rows[:, g, :, :], in_=gate_hidden_weight[g].rearrange("(half p) k -> p half k", p=P)
+            )
 
         w_codes = consts.tile([P, GATES, 4 * CH], U8, align_bytes=64)
         for g in range(GATES):
+            rows = gate_scales[g].rearrange("o q n -> (o q) n")
+            for quadrant in range(4):
+                nc.sync.dma_start(
+                    out=w_planes[32 * quadrant : 32 * quadrant + 4, g * CH : (g + 1) * CH].bitcast(I32),
+                    in_=rows[4 * quadrant : 4 * quadrant + 4, :].bitcast(I32),
+                )
             nc.sync.dma_start(
                 out=w_codes[:, g, :].bitcast(I32),
                 in_=gate_words[g].rearrange("o p n t -> (o p) (n t)").bitcast(I32),
             )
 
-        bias = consts.tile([P, GATES, CH], BF16)
-        for g in range(GATES):
-            nc.scalar.dma_start(out=bias[:, g, :], in_=gate_b[g].partition_broadcast(P))
-
-        for c in range(1, TILES // CHUNK):
-            load_chunk(c)
-
-        uT = consts.tile([P, K_CHUNKS, GATES * CH], BF16)
-        for g in range(GATES):
-            uT_ps = psum_tr.tile([P, K_CHUNKS, K_CHUNKS, P], BF16, tag="hT_ps")
-            for kc in range(K_CHUNKS):
-                for half in range(K_CHUNKS):
-                    nc.tensor.transpose(
-                        uT_ps[:, kc, half, :], u_rows[:, g, half, kc * P : (kc + 1) * P], ident_bf16[:]
-                    )
-            nc.scalar.copy(
-                out=uT[:, :, g * CH : (g + 1) * CH], in_=uT_ps[:].rearrange("p kc half n -> p kc (half n)")
-            )
+        load_operands(1)
+        for q in range(QUADS):
+            load_cells(q)
+            if q + 2 < QUADS:
+                load_operands(q + 2)
 
         zT_ps = {}
         hT_ps = {}
@@ -133,29 +136,29 @@ def tile_treelstm_pb_t_kernel(
         hT = {}
         z_codes = {}
         z_planes = {}
+        mx_ps = {}
+        mxT = {}
+        gate_ps = {}
         gates = {}
+        iu = {}
         res = {}
         tanh_c = {}
-        plain_ps = {}
-        mx_ps = {}
-        pre = {}
-        iu = {}
 
-        def chunk_rows(tiles_sb, j):
-            first = (j * PAIR) % CHUNK
-            return tiles_sb[(j * PAIR) // CHUNK][:, first : first + PAIR, :]
+        def pair_rows(tiles_sb, j):
+            first = (j * PAIR) % QUAD
+            return tiles_sb[(j * PAIR) // QUAD][:, first : first + PAIR, :]
 
         def transpose_pair(j):
             zT_ps[j] = psum_tr.tile([P, PAIR, 2, P], F32, tag="zT_ps", name="zT_ps")
             for a in range(PAIR):
-                words = chunk_rows(z_sb, j)[:, a, :].bitcast(F32)
+                words = pair_rows(z_sb, j)[:, a, :].bitcast(F32)
                 for u in range(2):
                     nc.tensor.transpose(zT_ps[j][:, a, u, :], words[:, u : FEAT // 2 : 2], ident_f32[:])
-            hT_ps[j] = psum_tr.tile([P, PAIR, K_CHUNKS, P], BF16, tag="hT_ps", name="hT_ps")
+            hT_ps[j] = psum_tr.tile([P, PAIR, HALVES, P], BF16, tag="hT_ps", name="hT_ps")
             for a in range(PAIR):
-                for kc in range(K_CHUNKS):
+                for kc in range(HALVES):
                     nc.tensor.transpose(
-                        hT_ps[j][:, a, kc, :], chunk_rows(h_sb, j)[:, a, kc * P : (kc + 1) * P], ident_bf16[:]
+                        hT_ps[j][:, a, kc, :], pair_rows(h_sb, j)[:, a, kc * P : (kc + 1) * P], ident_bf16[:]
                     )
 
         def copy_out(j):
@@ -164,73 +167,78 @@ def tile_treelstm_pb_t_kernel(
                 out=grouped[j][:].bitcast(F32).rearrange("p (a n u) -> p a n u", a=PAIR, u=2),
                 in_=zT_ps[j][:].rearrange("p a u n -> p a n u"),
             )
-            hT[j] = work.tile([P, PAIR, K_CHUNKS, P], BF16, tag="hT", name="hT")
+            hT[j] = ahead.tile([P, PAIR, HALVES, P], BF16, tag="hT", name="hT")
             nc.scalar.copy(out=hT[j][:], in_=hT_ps[j][:])
 
         def quantise(j):
-            z_codes[j] = work.tile([P, PAIR * P], U32, align_bytes=64, tag="z_codes", name="z_codes")
-            z_planes[j] = work.tile([P, PAIR * P], U8, align_bytes=64, tag="z_planes", name="z_planes")
-            nc.vector.quantize_mx(out=z_codes[j][:].bitcast(FP8X4), scales=z_planes[j][:], in_=grouped[j][:])
-
-        def plain_product(j, g):
-            bank = psum_prod.tile([P, PAIR, CH], F32, tag="plain_ps")
-            for a in range(PAIR):
-                for kc in range(K_CHUNKS):
-                    nc.tensor.matmul(
-                        bank[:, a, :],
-                        lhsT=hT[j][:, a, kc, :],
-                        rhs=uT[:, kc, g * CH : (g + 1) * CH],
-                        start=(kc == 0),
-                        stop=(kc == K_CHUNKS - 1),
-                    )
-            return bank
-
-        def mx_product(j, g):
-            bank = psum_prod.tile([P, PAIR, CH], F32, tag="mx_ps")
-            for a in range(PAIR):
-                nodes = slice(a * P, (a + 1) * P)
-                nc.tensor.matmul_mx(
-                    out=bank[:, a, :],
-                    lhsT=z_codes[j][:, nodes].bitcast(FP8X4),
-                    lhsT_scale=z_planes[j][:, nodes],
-                    rhs=w_codes[:, g, :].bitcast(FP8X4),
-                    rhs_scale=w_planes[:, g * CH : (g + 1) * CH],
-                    start=True,
-                    stop=True,
-                )
-            return bank
-
-        def products(j, g):
-            if g == GATES - 1:
-                mx_ps[j, g] = mx_product(j, g)
-                plain_ps[j, g] = plain_product(j, g)
-            else:
-                plain_ps[j, g] = plain_product(j, g)
-                mx_ps[j, g] = mx_product(j, g)
-
-        def add_bias(j, g):
-            pre[j, g] = work.tile([P, PAIR, CH], F32, tag="pre", name="pre")
-            nc.vector.tensor_tensor(
-                out=pre[j, g][:],
-                in0=plain_ps[j, g][:],
-                in1=bias[:, g, :].unsqueeze(1).to_broadcast([P, PAIR, CH]),
-                op=ALU.add,
+            q = j * PAIR // QUAD
+            if j * PAIR % QUAD == 0:
+                z_codes[q] = quads.tile([P, QUAD * P], U32, align_bytes=64, tag="z_codes", name="z_codes")
+                z_planes[q] = quads.tile([P, QUAD * P], U8, align_bytes=64, tag="z_planes", name="z_planes")
+            nodes = slice(j * PAIR % QUAD * P, (j * PAIR % QUAD + PAIR) * P)
+            nc.vector.quantize_mx(
+                out=z_codes[q][:, nodes].bitcast(FP8X4), scales=z_planes[q][:, nodes], in_=grouped[j][:]
             )
 
-        def finish_gate(j, g):
-            nc.vector.tensor_tensor(out=pre[j, g][:], in0=mx_ps[j, g][:], in1=pre[j, g][:], op=ALU.add)
+        def mx_block(q, b):
+            mx_ps[q, b] = psum_mx.tile([P, QUAD * P], F32, tag="mx_ps", name="mx_ps")
+            nc.tensor.matmul_mx(
+                out=mx_ps[q, b][:],
+                lhsT=w_codes[:, b // HALVES, (b % HALVES) * 4 * P : (b % HALVES + 1) * 4 * P].bitcast(FP8X4),
+                lhsT_scale=w_planes[:, b * P : (b + 1) * P],
+                rhs=z_codes[q][:].bitcast(FP8X4),
+                rhs_scale=z_planes[q][:],
+                start=True,
+                stop=True,
+            )
+
+        def block_out(q, b):
+            mxT[q, b] = blocks.tile([P, QUAD * P], F32, tag="mxT%d" % b, name="mxT%d" % b)
+            if b % GATES == GATES - 1:
+                nc.scalar.activation(
+                    out=mxT[q, b][:], in_=mx_ps[q, b][:], func=ACT.Identity, bias=bias_cols[:, b : b + 1]
+                )
+            else:
+                nc.vector.tensor_scalar(
+                    out=mxT[q, b][:], in0=mx_ps[q, b][:], scalar1=bias_cols[:, b : b + 1], scalar2=None, op0=ALU.add
+                )
+
+        def gate_argument(j, g, next_block):
+            q = j * PAIR // QUAD
+            gate_ps[j, g] = psum_gate.tile([P, PAIR, CH], F32, tag="gate_ps", name="gate_ps")
+            for a in range(PAIR):
+                nodes = slice((j * PAIR % QUAD + a) * P, (j * PAIR % QUAD + a + 1) * P)
+                for half in range(HALVES):
+                    nc.tensor.matmul(
+                        gate_ps[j, g][:, a, half * P : (half + 1) * P],
+                        lhsT=mxT[q, HALVES * g + half][:, nodes],
+                        rhs=ident_f32[:],
+                        is_transpose=True,
+                        start=(half == 0),
+                        stop=False,
+                    )
+                for kc in range(HALVES):
+                    if a == PAIR - 1 and kc == HALVES - 1 and next_block is not None:
+                        mx_block(*next_block)
+                    nc.tensor.matmul(
+                        gate_ps[j, g][:, a, :],
+                        lhsT=hT[j][:, a, kc, :],
+                        rhs=uT[:, kc, g * CH : (g + 1) * CH],
+                        start=False,
+                        stop=(kc == HALVES - 1),
+                    )
+
+        def squash_gate(j, g):
             gates[j, g] = work.tile([P, PAIR, CH], F32, tag="gate%d" % g, name="gate%d" % g)
-            nc.scalar.activation(out=gates[j, g][:], in_=pre[j, g][:], func=gate_func[g])
+            nc.scalar.activation(out=gates[j, g][:], in_=gate_ps[j, g][:], func=gate_func[g])
 
         def input_times_update(j):
             iu[j] = work.tile([P, PAIR, CH], F32, tag="iu", name="iu")
-            nc.gpsimd.tensor_tensor(out=iu[j][:], in0=gates[j, 0][:], in1=gates[j, 1][:], op=ALU.mult)
+            nc.vector.tensor_tensor(out=iu[j][:], in0=gates[j, 0][:], in1=gates[j, 1][:], op=ALU.mult)
 
         def cell(j):
             res[j] = results.tile([P, PAIR, 2 * CH], F32, tag="res", name="res")
-            nc.gpsimd.tensor_tensor(out=res[j][:, :, CH:], in0=iu[j][:], in1=chunk_rows(fc_sb, j), op=ALU.add)
-
-        def squash_cell(j):
+            nc.vector.tensor_tensor(out=res[j][:, :, CH:], in0=iu[j][:], in1=pair_rows(fc_sb, j), op=ALU.add)
             tanh_c[j] = work.tile([P, PAIR, CH], F32, tag="tanh_c", name="tanh_c")
             nc.scalar.activation(out=tanh_c[j][:], in_=res[j][:, :, CH:], func=ACT.Tanh)
 
@@ -239,35 +247,51 @@ def tile_treelstm_pb_t_kernel(
             nc.sync.dma_start(out=out_view[:, j * PAIR : (j + 1) * PAIR, :], in_=res[j][:])
 
         with tc.manual_schedule():
-            for j in range(2):
+            for j in range(PAIR):
                 transpose_pair(j)
                 copy_out(j)
-            quantise(0)
-            products(0, 0)
-            add_bias(0, 0)
-            for j in range(PAIRS):
-                products(j, 1)
-                add_bias(j, 1)
-                finish_gate(j, 0)
-                if j + 1 < PAIRS:
-                    quantise(j + 1)
+                quantise(j)
 
-                products(j, 2)
-                if j + 2 < PAIRS:
-                    transpose_pair(j + 2)
-                add_bias(j, 2)
-                finish_gate(j, 1)
-                input_times_update(j)
-                if j > 0:
-                    squash_cell(j - 1)
-                    hidden(j - 1)
+            bias_ps = psum_tr.tile([P, P], BF16, tag="hT_ps")
+            nc.tensor.transpose(bias_ps[:], bias_rows[:], ident_bf16[:])
+            bias_cols = consts.tile([P, BLOCKS], F32)
+            nc.vector.tensor_copy(out=bias_cols[:], in_=bias_ps[:, :BLOCKS])
 
-                if j + 2 < PAIRS:
-                    copy_out(j + 2)
-                if j + 1 < PAIRS:
-                    products(j + 1, 0)
-                    add_bias(j + 1, 0)
-                finish_gate(j, 2)
-                cell(j)
-            squash_cell(PAIRS - 1)
+            uT = consts.tile([P, HALVES, GATES * CH], BF16)
+            for g in range(GATES):
+                uT_ps = psum_tr.tile([P, HALVES, HALVES, P], BF16, tag="hT_ps")
+                for kc in range(HALVES):
+                    for half in range(HALVES):
+                        nc.tensor.transpose(
+                            uT_ps[:, kc, half, :], u_rows[:, g, half, kc * P : (kc + 1) * P], ident_bf16[:]
+                        )
+                nc.vector.tensor_copy(
+                    out=uT[:, :, g * CH : (g + 1) * CH], in_=uT_ps[:].rearrange("p kc half n -> p kc (half n)")
+                )
+
+            for j in range(-PAIR, PAIRS):
+                next_quad = (j + PAIR) * PAIR // QUAD
+                for g in range(GATES):
+                    next_block = (next_quad, (j * GATES + g) % BLOCKS) if next_quad < QUADS else None
+                    if g == 0 and j > 0:
+                        cell(j - 1)
+                    if g == 1 and j > 0:
+                        hidden(j - 1)
+                    if j >= 0:
+                        gate_argument(j, g, next_block)
+                    else:
+                        mx_block(*next_block)
+                    if g == 0 and j + AHEAD < PAIRS:
+                        transpose_pair(j + AHEAD)
+                    if j >= 0:
+                        squash_gate(j, g)
+                    if next_block is not None:
+                        block_out(*next_block)
+                    if g == 0 and j + AHEAD < PAIRS:
+                        copy_out(j + AHEAD)
+                if j >= 0:
+                    input_times_update(j)
+                if j + AHEAD < PAIRS:
+                    quantise(j + AHEAD)
+            cell(PAIRS - 1)
             hidden(PAIRS - 1)

@@ -24,6 +24,8 @@ QUAD = 4
 QUADS = TILES // QUAD
 GATES = 3
 BLOCKS = GATES * HALVES
+BANKS = PAIRS * GATES
+PIECES = PAIR * HALVES
 AHEAD = 4
 
 FLOPS = 2 * NODES * GATES * CH * (FEAT + CH)
@@ -69,7 +71,7 @@ def tile_treelstm_pb_t_kernel(
         work = ctx.enter_context(tc.tile_pool(name="work", bufs=3))
         results = ctx.enter_context(tc.tile_pool(name="results", bufs=4))
         psum_tr = ctx.enter_context(tc.psum_pool(name="psum_tr", bufs=1))
-        psum_mx = ctx.enter_context(tc.psum_pool(name="psum_mx", bufs=2))
+        psum_mx = ctx.enter_context(tc.psum_pool(name="psum_mx", bufs=GATES))
         psum_gate = ctx.enter_context(tc.psum_pool(name="psum_gate", bufs=4))
 
         w_planes = consts.tile([P, GATES * CH], U8, align_bytes=64)
@@ -148,27 +150,39 @@ def tile_treelstm_pb_t_kernel(
             first = (j * PAIR) % QUAD
             return tiles_sb[(j * PAIR) // QUAD][:, first : first + PAIR, :]
 
-        def transpose_pair(j):
-            zT_ps[j] = psum_tr.tile([P, PAIR, 2, P], F32, tag="zT_ps", name="zT_ps")
+        def transpose_bank(j, dtype):
+            if j < AHEAD:
+                return psum_gate.tile([P, PAIR, 2, P], dtype, tag="gate_ps", name="early_ps")
+            return psum_tr.tile([P, PAIR, 2, P], dtype, tag="tr_ps", name="late_ps")
+
+        def transpose_z(j):
+            zT_ps[j] = transpose_bank(j, F32)
             for a in range(PAIR):
                 words = pair_rows(z_sb, j)[:, a, :].bitcast(F32)
                 for u in range(2):
                     nc.tensor.transpose(zT_ps[j][:, a, u, :], words[:, u : FEAT // 2 : 2], ident_f32[:])
-            hT_ps[j] = psum_tr.tile([P, PAIR, HALVES, P], BF16, tag="hT_ps", name="hT_ps")
+
+        def copy_z(j):
+            grouped[j] = work.tile([P, PAIR * P * 4], BF16, align_bytes=64, tag="grouped", name="grouped")
+            nc.scalar.copy(
+                out=grouped[j][:].bitcast(F32).rearrange("p (a n u) -> p a n u", a=PAIR, u=2),
+                in_=zT_ps[j][:].rearrange("p a u n -> p a n u"),
+            )
+
+        def transpose_h(j):
+            hT_ps[j] = transpose_bank(j, BF16)
             for a in range(PAIR):
                 for kc in range(HALVES):
                     nc.tensor.transpose(
                         hT_ps[j][:, a, kc, :], pair_rows(h_sb, j)[:, a, kc * P : (kc + 1) * P], ident_bf16[:]
                     )
 
-        def copy_out(j):
-            grouped[j] = work.tile([P, PAIR * P * 4], BF16, align_bytes=64, tag="grouped", name="grouped")
-            nc.scalar.copy(
-                out=grouped[j][:].bitcast(F32).rearrange("p (a n u) -> p a n u", a=PAIR, u=2),
-                in_=zT_ps[j][:].rearrange("p a u n -> p a n u"),
-            )
+        def copy_h(j):
             hT[j] = ahead.tile([P, PAIR, HALVES, P], BF16, tag="hT", name="hT")
-            nc.scalar.copy(out=hT[j][:], in_=hT_ps[j][:])
+            if j < AHEAD:
+                nc.vector.tensor_copy(out=hT[j][:], in_=hT_ps[j][:])
+            else:
+                nc.scalar.copy(out=hT[j][:], in_=hT_ps[j][:])
 
         def quantise(j):
             q = j * PAIR // QUAD
@@ -194,7 +208,7 @@ def tile_treelstm_pb_t_kernel(
 
         def block_out(q, b):
             mxT[q, b] = blocks.tile([P, QUAD * P], F32, tag="mxT%d" % b, name="mxT%d" % b)
-            if b % GATES == GATES - 1:
+            if b == BLOCKS - 1:
                 nc.scalar.activation(
                     out=mxT[q, b][:], in_=mx_ps[q, b][:], func=ACT.Identity, bias=bias_cols[:, b : b + 1]
                 )
@@ -203,38 +217,39 @@ def tile_treelstm_pb_t_kernel(
                     out=mxT[q, b][:], in0=mx_ps[q, b][:], scalar1=bias_cols[:, b : b + 1], scalar2=None, op0=ALU.add
                 )
 
-        def gate_argument(j, g, next_block):
-            q = j * PAIR // QUAD
-            gate_ps[j, g] = psum_gate.tile([P, PAIR, CH], F32, tag="gate_ps", name="gate_ps")
-            for a in range(PAIR):
-                nodes = slice((j * PAIR % QUAD + a) * P, (j * PAIR % QUAD + a + 1) * P)
-                for half in range(HALVES):
-                    nc.tensor.matmul(
-                        gate_ps[j, g][:, a, half * P : (half + 1) * P],
-                        lhsT=mxT[q, HALVES * g + half][:, nodes],
-                        rhs=ident_f32[:],
-                        is_transpose=True,
-                        start=(half == 0),
-                        stop=False,
-                    )
-                for kc in range(HALVES):
-                    if a == PAIR - 1 and kc == HALVES - 1 and next_block is not None:
-                        mx_block(*next_block)
-                    nc.tensor.matmul(
-                        gate_ps[j, g][:, a, :],
-                        lhsT=hT[j][:, a, kc, :],
-                        rhs=uT[:, kc, g * CH : (g + 1) * CH],
-                        start=False,
-                        stop=(kc == HALVES - 1),
-                    )
+        def bring_in(s, i):
+            j, g = divmod(s, GATES)
+            a, half = divmod(i, HALVES)
+            if i == 0:
+                gate_ps[s] = psum_gate.tile([P, PAIR, CH], F32, tag="gate_ps", name="gate_ps")
+            nodes = slice((j * PAIR % QUAD + a) * P, (j * PAIR % QUAD + a + 1) * P)
+            nc.tensor.matmul(
+                gate_ps[s][:, a, half * P : (half + 1) * P],
+                lhsT=mxT[j * PAIR // QUAD, HALVES * g + half][:, nodes],
+                rhs=ident_f32[:],
+                is_transpose=True,
+                start=(i == 0),
+                stop=False,
+            )
 
-        def squash_gate(j, g):
-            gates[j, g] = work.tile([P, PAIR, CH], F32, tag="gate%d" % g, name="gate%d" % g)
-            nc.scalar.activation(out=gates[j, g][:], in_=gate_ps[j, g][:], func=gate_func[g])
+        def add_hidden(s, i):
+            j, g = divmod(s, GATES)
+            a, kc = divmod(i, HALVES)
+            nc.tensor.matmul(
+                gate_ps[s][:, a, :],
+                lhsT=hT[j][:, a, kc, :],
+                rhs=uT[:, kc, g * CH : (g + 1) * CH],
+                start=False,
+                stop=(i == PIECES - 1),
+            )
+
+        def squash_gate(s):
+            gates[s] = work.tile([P, PAIR, CH], F32, tag="gate%d" % (s % GATES), name="gate%d" % (s % GATES))
+            nc.scalar.activation(out=gates[s][:], in_=gate_ps[s][:], func=gate_func[s % GATES])
 
         def input_times_update(j):
             iu[j] = work.tile([P, PAIR, CH], F32, tag="iu", name="iu")
-            nc.vector.tensor_tensor(out=iu[j][:], in0=gates[j, 0][:], in1=gates[j, 1][:], op=ALU.mult)
+            nc.vector.tensor_tensor(out=iu[j][:], in0=gates[GATES * j][:], in1=gates[GATES * j + 1][:], op=ALU.mult)
 
         def cell(j):
             res[j] = results.tile([P, PAIR, 2 * CH], F32, tag="res", name="res")
@@ -243,23 +258,26 @@ def tile_treelstm_pb_t_kernel(
             nc.scalar.activation(out=tanh_c[j][:], in_=res[j][:, :, CH:], func=ACT.Tanh)
 
         def hidden(j):
-            nc.vector.tensor_tensor(out=res[j][:, :, :CH], in0=gates[j, 2][:], in1=tanh_c[j][:], op=ALU.mult)
+            nc.vector.tensor_tensor(out=res[j][:, :, :CH], in0=gates[GATES * j + 2][:], in1=tanh_c[j][:], op=ALU.mult)
             nc.sync.dma_start(out=out_view[:, j * PAIR : (j + 1) * PAIR, :], in_=res[j][:])
 
         with tc.manual_schedule():
-            for j in range(PAIR):
-                transpose_pair(j)
-                copy_out(j)
+            for j in range(QUAD // PAIR):
+                transpose_z(j)
+                copy_z(j)
+            for j in range(QUAD // PAIR):
                 quantise(j)
+                transpose_h(j)
+                copy_h(j)
 
-            bias_ps = psum_tr.tile([P, P], BF16, tag="hT_ps")
+            bias_ps = psum_gate.tile([P, P], BF16, tag="gate_ps")
             nc.tensor.transpose(bias_ps[:], bias_rows[:], ident_bf16[:])
             bias_cols = consts.tile([P, BLOCKS], F32)
             nc.vector.tensor_copy(out=bias_cols[:], in_=bias_ps[:, :BLOCKS])
 
             uT = consts.tile([P, HALVES, GATES * CH], BF16)
             for g in range(GATES):
-                uT_ps = psum_tr.tile([P, HALVES, HALVES, P], BF16, tag="hT_ps")
+                uT_ps = psum_gate.tile([P, HALVES, HALVES, P], BF16, tag="gate_ps")
                 for kc in range(HALVES):
                     for half in range(HALVES):
                         nc.tensor.transpose(
@@ -269,26 +287,36 @@ def tile_treelstm_pb_t_kernel(
                     out=uT[:, :, g * CH : (g + 1) * CH], in_=uT_ps[:].rearrange("p kc half n -> p kc (half n)")
                 )
 
-            for j in range(-PAIR, PAIRS):
-                next_quad = (j + PAIR) * PAIR // QUAD
+            for j in range(-(QUAD // PAIR), PAIRS):
+                next_quad = (j * PAIR + QUAD) // QUAD
+                run = [(next_quad, j % (QUAD // PAIR) * GATES + r) for r in range(GATES)] if next_quad < QUADS else []
                 for g in range(GATES):
-                    next_block = (next_quad, (j * GATES + g) % BLOCKS) if next_quad < QUADS else None
+                    s = j * GATES + g
                     if g == 0 and j > 0:
                         cell(j - 1)
                     if g == 1 and j > 0:
                         hidden(j - 1)
+                    for i in range(PIECES):
+                        if j >= 0:
+                            add_hidden(s, i)
+                        if i == PIECES - 1 and g == 0:
+                            for block in run:
+                                mx_block(*block)
+                            if j + AHEAD < PAIRS:
+                                transpose_z(j + AHEAD)
+                        if i == PIECES - 1 and g == GATES - 1 and j + AHEAD < PAIRS:
+                            transpose_h(j + AHEAD)
+                        if 0 <= s + 1 < BANKS:
+                            bring_in(s + 1, i)
                     if j >= 0:
-                        gate_argument(j, g, next_block)
-                    else:
-                        mx_block(*next_block)
-                    if g == 0 and j + AHEAD < PAIRS:
-                        transpose_pair(j + AHEAD)
-                    if j >= 0:
-                        squash_gate(j, g)
-                    if next_block is not None:
-                        block_out(*next_block)
-                    if g == 0 and j + AHEAD < PAIRS:
-                        copy_out(j + AHEAD)
+                        squash_gate(s)
+                    if g == 0:
+                        for block in run:
+                            block_out(*block)
+                        if j + AHEAD < PAIRS:
+                            copy_z(j + AHEAD)
+                if j + AHEAD < PAIRS:
+                    copy_h(j + AHEAD)
                 if j >= 0:
                     input_times_update(j)
                 if j + AHEAD < PAIRS:

@@ -71,7 +71,7 @@ def tile_treelstm_pb_t_kernel(
         work = ctx.enter_context(tc.tile_pool(name="work", bufs=3))
         results = ctx.enter_context(tc.tile_pool(name="results", bufs=4))
         psum_tr = ctx.enter_context(tc.psum_pool(name="psum_tr", bufs=1))
-        psum_mx = ctx.enter_context(tc.psum_pool(name="psum_mx", bufs=GATES))
+        psum_mx = ctx.enter_context(tc.psum_pool(name="psum_mx", bufs=2))
         psum_gate = ctx.enter_context(tc.psum_pool(name="psum_gate", bufs=4))
 
         w_planes = consts.tile([P, GATES * CH], U8, align_bytes=64)
@@ -150,13 +150,13 @@ def tile_treelstm_pb_t_kernel(
             first = (j * PAIR) % QUAD
             return tiles_sb[(j * PAIR) // QUAD][:, first : first + PAIR, :]
 
-        def transpose_bank(j, dtype):
+        def transpose_bank(j, dtype, tag):
             if j < AHEAD:
                 return psum_gate.tile([P, PAIR, 2, P], dtype, tag="gate_ps", name="early_ps")
-            return psum_tr.tile([P, PAIR, 2, P], dtype, tag="tr_ps", name="late_ps")
+            return psum_tr.tile([P, PAIR, 2, P], dtype, tag=tag, name="late_ps")
 
         def transpose_z(j):
-            zT_ps[j] = transpose_bank(j, F32)
+            zT_ps[j] = transpose_bank(j, F32, "zT_ps")
             for a in range(PAIR):
                 words = pair_rows(z_sb, j)[:, a, :].bitcast(F32)
                 for u in range(2):
@@ -170,7 +170,7 @@ def tile_treelstm_pb_t_kernel(
             )
 
         def transpose_h(j):
-            hT_ps[j] = transpose_bank(j, BF16)
+            hT_ps[j] = transpose_bank(j, BF16, "hT_ps")
             for a in range(PAIR):
                 for kc in range(HALVES):
                     nc.tensor.transpose(
@@ -254,6 +254,8 @@ def tile_treelstm_pb_t_kernel(
         def cell(j):
             res[j] = results.tile([P, PAIR, 2 * CH], F32, tag="res", name="res")
             nc.vector.tensor_tensor(out=res[j][:, :, CH:], in0=iu[j][:], in1=pair_rows(fc_sb, j), op=ALU.add)
+
+        def squash_cell(j):
             tanh_c[j] = work.tile([P, PAIR, CH], F32, tag="tanh_c", name="tanh_c")
             nc.scalar.activation(out=tanh_c[j][:], in_=res[j][:, :, CH:], func=ACT.Tanh)
 
@@ -289,37 +291,35 @@ def tile_treelstm_pb_t_kernel(
 
             for j in range(-(QUAD // PAIR), PAIRS):
                 next_quad = (j * PAIR + QUAD) // QUAD
-                run = [(next_quad, j % (QUAD // PAIR) * GATES + r) for r in range(GATES)] if next_quad < QUADS else []
+                if j + AHEAD < PAIRS:
+                    transpose_z(j + AHEAD)
+                    transpose_h(j + AHEAD)
+                    copy_z(j + AHEAD)
+                    copy_h(j + AHEAD)
+                if j > 0:
+                    cell(j - 1)
+                    squash_cell(j - 1)
+                if j >= 0:
+                    for g in range(GATES):
+                        for i in range(PIECES):
+                            bring_in(j * GATES + g, i)
                 for g in range(GATES):
                     s = j * GATES + g
-                    if g == 0 and j > 0:
-                        cell(j - 1)
-                    if g == 1 and j > 0:
-                        hidden(j - 1)
                     for i in range(PIECES):
+                        if i == PIECES - 1 and next_quad < QUADS:
+                            mx_block(next_quad, s % BLOCKS)
                         if j >= 0:
                             add_hidden(s, i)
-                        if i == PIECES - 1 and g == 0:
-                            for block in run:
-                                mx_block(*block)
-                            if j + AHEAD < PAIRS:
-                                transpose_z(j + AHEAD)
-                        if i == PIECES - 1 and g == GATES - 1 and j + AHEAD < PAIRS:
-                            transpose_h(j + AHEAD)
-                        if 0 <= s + 1 < BANKS:
-                            bring_in(s + 1, i)
                     if j >= 0:
                         squash_gate(s)
-                    if g == 0:
-                        for block in run:
-                            block_out(*block)
-                        if j + AHEAD < PAIRS:
-                            copy_z(j + AHEAD)
-                if j + AHEAD < PAIRS:
-                    copy_h(j + AHEAD)
-                if j >= 0:
-                    input_times_update(j)
-                if j + AHEAD < PAIRS:
-                    quantise(j + AHEAD)
+                    if next_quad < QUADS:
+                        block_out(next_quad, s % BLOCKS)
+                    if g == 0 and j > 0:
+                        hidden(j - 1)
+                    if g == 1 and j >= 0:
+                        input_times_update(j)
+                    if g == 2 and j + AHEAD < PAIRS:
+                        quantise(j + AHEAD)
             cell(PAIRS - 1)
+            squash_cell(PAIRS - 1)
             hidden(PAIRS - 1)

@@ -23,10 +23,13 @@ PAIRS = TILES // PAIR
 QUAD = 4
 QUADS = TILES // QUAD
 GATES = 3
-BLOCKS = GATES * HALVES
-BANKS = PAIRS * GATES
+GATE_I = 0
+GATE_U = 1
+GATE_O = 2
+BLOCKS = 2 * HALVES
 PIECES = PAIR * HALVES
-AHEAD = 4
+Z_AHEAD = 5
+H_AHEAD = 2
 
 FLOPS = 2 * NODES * GATES * CH * (FEAT + CH)
 
@@ -54,7 +57,6 @@ def tile_treelstm_pb_t_kernel(
     gate_words = [W_i_words, W_u_words, W_o_words]
     gate_scales = [W_i_scales, W_u_scales, W_o_scales]
     gate_hidden_weight = [U_i, U_u, U_o]
-    gate_bias = [b_i, b_u, b_o]
     gate_func = [ACT.Sigmoid, ACT.Tanh, ACT.Sigmoid]
 
     z_view = z0.rearrange("(p t) k -> p t k", t=TILES)
@@ -65,14 +67,11 @@ def tile_treelstm_pb_t_kernel(
     with ExitStack() as ctx:
         consts = ctx.enter_context(tc.tile_pool(name="consts", bufs=1))
         inputs = ctx.enter_context(tc.tile_pool(name="inputs", bufs=1))
-        ahead = ctx.enter_context(tc.tile_pool(name="ahead", bufs=AHEAD + 2))
         quads = ctx.enter_context(tc.tile_pool(name="quads", bufs=3))
         blocks = ctx.enter_context(tc.tile_pool(name="blocks", bufs=2))
-        work = ctx.enter_context(tc.tile_pool(name="work", bufs=3))
-        results = ctx.enter_context(tc.tile_pool(name="results", bufs=4))
-        psum_tr = ctx.enter_context(tc.psum_pool(name="psum_tr", bufs=1))
-        psum_mx = ctx.enter_context(tc.psum_pool(name="psum_mx", bufs=2))
-        psum_gate = ctx.enter_context(tc.psum_pool(name="psum_gate", bufs=4))
+        work = ctx.enter_context(tc.tile_pool(name="work", bufs=4))
+        psum_one = ctx.enter_context(tc.psum_pool(name="psum_one", bufs=1))
+        psum_two = ctx.enter_context(tc.psum_pool(name="psum_two", bufs=2))
 
         w_planes = consts.tile([P, GATES * CH], U8, align_bytes=64)
         nc.vector.memset(w_planes[:].bitcast(I32), 0)
@@ -92,29 +91,20 @@ def tile_treelstm_pb_t_kernel(
             h_sb.append(inputs.tile([P, QUAD, CH], BF16, name="h_sb%d" % q))
             fc_sb.append(inputs.tile([P, QUAD, CH], BF16, name="fc_sb%d" % q))
 
-        def load_operands(q):
-            nc.sync.dma_start(out=z_sb[q][:], in_=z_view[:, q * QUAD : (q + 1) * QUAD, :])
-            nc.sync.dma_start(out=h_sb[q][:], in_=h_view[:, q * QUAD : (q + 1) * QUAD, :])
+        def load(tiles_sb, view, q):
+            if q < QUADS:
+                nc.sync.dma_start(out=tiles_sb[q][:], in_=view[:, q * QUAD : (q + 1) * QUAD, :])
 
-        def load_cells(q):
-            nc.sync.dma_start(out=fc_sb[q][:], in_=fc_view[:, q * QUAD : (q + 1) * QUAD, :])
-
-        for g in range(GATES):
+        for g, bias in ((GATE_I, b_i), (GATE_U, b_u)):
             nc.scalar.dma_start(
-                out=bias_rows[HALVES * g : HALVES * (g + 1), :],
-                in_=gate_bias[g].rearrange("(half c) -> half c", c=P),
+                out=bias_rows[HALVES * g : HALVES * (g + 1), :], in_=bias.rearrange("(half c) -> half c", c=P)
             )
-
-        load_operands(0)
-
-        u_rows = consts.tile([P, GATES, HALVES, CH], BF16)
-        for g in range(GATES):
-            nc.sync.dma_start(
-                out=u_rows[:, g, :, :], in_=gate_hidden_weight[g].rearrange("(half p) k -> p half k", p=P)
-            )
+        bias_o = consts.tile([P, CH], BF16)
+        nc.scalar.dma_start(out=bias_o[:], in_=b_o.partition_broadcast(P))
 
         w_codes = consts.tile([P, GATES, 4 * CH], U8, align_bytes=64)
-        for g in range(GATES):
+
+        def load_weight(g):
             rows = gate_scales[g].rearrange("o q n -> (o q) n")
             for quadrant in range(4):
                 nc.sync.dma_start(
@@ -126,11 +116,23 @@ def tile_treelstm_pb_t_kernel(
                 in_=gate_words[g].rearrange("o p n t -> (o p) (n t)").bitcast(I32),
             )
 
-        load_operands(1)
+        load(z_sb, z_view, 0)
+        load_weight(GATE_I)
+        load_weight(GATE_U)
+        load(z_sb, z_view, 1)
+        load(h_sb, h_view, 0)
+        u_rows = consts.tile([P, GATES, HALVES, CH], BF16)
+        for g in range(GATES):
+            nc.sync.dma_start(
+                out=u_rows[:, g, :, :], in_=gate_hidden_weight[g].rearrange("(half p) k -> p half k", p=P)
+            )
+        load_weight(GATE_O)
+        load(z_sb, z_view, 2)
+        load(h_sb, h_view, 1)
         for q in range(QUADS):
-            load_cells(q)
-            if q + 2 < QUADS:
-                load_operands(q + 2)
+            load(fc_sb, fc_view, q)
+            load(z_sb, z_view, q + 3)
+            load(h_sb, h_view, q + 2)
 
         zT_ps = {}
         hT_ps = {}
@@ -138,53 +140,49 @@ def tile_treelstm_pb_t_kernel(
         hT = {}
         z_codes = {}
         z_planes = {}
-        mx_ps = {}
-        mxT = {}
+        block_ps = {}
+        block_sb = {}
         gate_ps = {}
+        o_mx_ps = {}
+        o_sum = {}
         gates = {}
         iu = {}
         res = {}
         tanh_c = {}
 
+        def exists(j):
+            return 0 <= j < PAIRS
+
         def pair_rows(tiles_sb, j):
             first = (j * PAIR) % QUAD
             return tiles_sb[(j * PAIR) // QUAD][:, first : first + PAIR, :]
 
-        def transpose_bank(j, dtype, tag):
-            if j < AHEAD:
-                return psum_gate.tile([P, PAIR, 2, P], dtype, tag="gate_ps", name="early_ps")
-            return psum_tr.tile([P, PAIR, 2, P], dtype, tag=tag, name="late_ps")
+        def quad_columns(j, a):
+            return slice((j * PAIR % QUAD + a) * P, (j * PAIR % QUAD + a + 1) * P)
 
-        def transpose_z(j):
-            zT_ps[j] = transpose_bank(j, F32, "zT_ps")
-            for a in range(PAIR):
-                words = pair_rows(z_sb, j)[:, a, :].bitcast(F32)
-                for u in range(2):
-                    nc.tensor.transpose(zT_ps[j][:, a, u, :], words[:, u : FEAT // 2 : 2], ident_f32[:])
+        def transpose_z(j, i):
+            if not exists(j):
+                return
+            a, u = divmod(i, 2)
+            if i == 0 and j < Z_AHEAD - 1:
+                zT_ps[j] = psum_two.tile([P, PAIR, 2, P], F32, tag="gate_ps", name="zT_early_ps")
+            elif i == 0:
+                zT_ps[j] = psum_one.tile([P, PAIR, 2, P], F32, tag="zT_ps", name="zT_ps")
+            words = pair_rows(z_sb, j)[:, a, :].bitcast(F32)
+            nc.tensor.transpose(zT_ps[j][:, a, u, :], words[:, u : FEAT // 2 : 2], ident_f32[:])
 
         def copy_z(j):
+            if not exists(j):
+                return
             grouped[j] = work.tile([P, PAIR * P * 4], BF16, align_bytes=64, tag="grouped", name="grouped")
             nc.scalar.copy(
                 out=grouped[j][:].bitcast(F32).rearrange("p (a n u) -> p a n u", a=PAIR, u=2),
                 in_=zT_ps[j][:].rearrange("p a u n -> p a n u"),
             )
 
-        def transpose_h(j):
-            hT_ps[j] = transpose_bank(j, BF16, "hT_ps")
-            for a in range(PAIR):
-                for kc in range(HALVES):
-                    nc.tensor.transpose(
-                        hT_ps[j][:, a, kc, :], pair_rows(h_sb, j)[:, a, kc * P : (kc + 1) * P], ident_bf16[:]
-                    )
-
-        def copy_h(j):
-            hT[j] = ahead.tile([P, PAIR, HALVES, P], BF16, tag="hT", name="hT")
-            if j < AHEAD:
-                nc.vector.tensor_copy(out=hT[j][:], in_=hT_ps[j][:])
-            else:
-                nc.scalar.copy(out=hT[j][:], in_=hT_ps[j][:])
-
         def quantise(j):
+            if not exists(j):
+                return
             q = j * PAIR // QUAD
             if j * PAIR % QUAD == 0:
                 z_codes[q] = quads.tile([P, QUAD * P], U32, align_bytes=64, tag="z_codes", name="z_codes")
@@ -194,10 +192,26 @@ def tile_treelstm_pb_t_kernel(
                 out=z_codes[q][:, nodes].bitcast(FP8X4), scales=z_planes[q][:, nodes], in_=grouped[j][:]
             )
 
+        def transpose_h(j):
+            if not exists(j):
+                return
+            hT_ps[j] = psum_one.tile([P, PAIR, HALVES, P], BF16, tag="hT_ps", name="hT_ps")
+            for a in range(PAIR):
+                for kc in range(HALVES):
+                    nc.tensor.transpose(
+                        hT_ps[j][:, a, kc, :], pair_rows(h_sb, j)[:, a, kc * P : (kc + 1) * P], ident_bf16[:]
+                    )
+
+        def copy_h(j):
+            if not exists(j):
+                return
+            hT[j] = work.tile([P, PAIR, HALVES, P], BF16, tag="hT", name="hT")
+            nc.scalar.copy(out=hT[j][:], in_=hT_ps[j][:])
+
         def mx_block(q, b):
-            mx_ps[q, b] = psum_mx.tile([P, QUAD * P], F32, tag="mx_ps", name="mx_ps")
+            block_ps[q, b] = psum_two.tile([P, QUAD * P], F32, tag="block_ps", name="block_ps")
             nc.tensor.matmul_mx(
-                out=mx_ps[q, b][:],
+                out=block_ps[q, b][:],
                 lhsT=w_codes[:, b // HALVES, (b % HALVES) * 4 * P : (b % HALVES + 1) * 4 * P].bitcast(FP8X4),
                 lhsT_scale=w_planes[:, b * P : (b + 1) * P],
                 rhs=z_codes[q][:].bitcast(FP8X4),
@@ -207,79 +221,129 @@ def tile_treelstm_pb_t_kernel(
             )
 
         def block_out(q, b):
-            mxT[q, b] = blocks.tile([P, QUAD * P], F32, tag="mxT%d" % b, name="mxT%d" % b)
-            if b == BLOCKS - 1:
-                nc.scalar.activation(
-                    out=mxT[q, b][:], in_=mx_ps[q, b][:], func=ACT.Identity, bias=bias_cols[:, b : b + 1]
+            block_sb[q, b] = blocks.tile([P, QUAD * P], F32, tag="block_sb%d" % b, name="block_sb%d" % b)
+            if b % 2 == 0:
+                nc.vector.tensor_scalar(
+                    out=block_sb[q, b][:],
+                    in0=block_ps[q, b][:],
+                    scalar1=bias_cols[:, b : b + 1],
+                    scalar2=None,
+                    op0=ALU.add,
                 )
             else:
-                nc.vector.tensor_scalar(
-                    out=mxT[q, b][:], in0=mx_ps[q, b][:], scalar1=bias_cols[:, b : b + 1], scalar2=None, op0=ALU.add
+                nc.scalar.activation(
+                    out=block_sb[q, b][:], in_=block_ps[q, b][:], func=ACT.Identity, bias=bias_cols[:, b : b + 1]
                 )
 
-        def bring_in(s, i):
-            j, g = divmod(s, GATES)
+        def bring_in(j, g, i):
+            if not exists(j):
+                return
             a, half = divmod(i, HALVES)
             if i == 0:
-                gate_ps[s] = psum_gate.tile([P, PAIR, CH], F32, tag="gate_ps", name="gate_ps")
-            nodes = slice((j * PAIR % QUAD + a) * P, (j * PAIR % QUAD + a + 1) * P)
+                gate_ps[j, g] = psum_two.tile([P, PAIR, CH], F32, tag="gate_ps", name="gate_ps")
             nc.tensor.matmul(
-                gate_ps[s][:, a, half * P : (half + 1) * P],
-                lhsT=mxT[j * PAIR // QUAD, HALVES * g + half][:, nodes],
+                gate_ps[j, g][:, a, half * P : (half + 1) * P],
+                lhsT=block_sb[j * PAIR // QUAD, HALVES * g + half][:, quad_columns(j, a)],
                 rhs=ident_f32[:],
                 is_transpose=True,
                 start=(i == 0),
                 stop=False,
             )
 
-        def add_hidden(s, i):
-            j, g = divmod(s, GATES)
+        def add_hidden(j, g, i):
+            if not exists(j):
+                return
             a, kc = divmod(i, HALVES)
+            if g == GATE_O and i == 0:
+                gate_ps[j, g] = psum_one.tile([P, PAIR, CH], F32, tag="o_plain_ps", name="o_plain_ps")
             nc.tensor.matmul(
-                gate_ps[s][:, a, :],
+                gate_ps[j, g][:, a, :],
                 lhsT=hT[j][:, a, kc, :],
                 rhs=uT[:, kc, g * CH : (g + 1) * CH],
-                start=False,
-                stop=(i == PIECES - 1),
+                start=(g == GATE_O and kc == 0),
+                stop=(kc == HALVES - 1 if g == GATE_O else i == PIECES - 1),
             )
 
-        def squash_gate(s):
-            gates[s] = work.tile([P, PAIR, CH], F32, tag="gate%d" % (s % GATES), name="gate%d" % (s % GATES))
-            nc.scalar.activation(out=gates[s][:], in_=gate_ps[s][:], func=gate_func[s % GATES])
+        def mx_o(j):
+            if not exists(j):
+                return
+            q = j * PAIR // QUAD
+            o_mx_ps[j] = psum_one.tile([P, PAIR, CH], F32, tag="o_mx_ps", name="o_mx_ps")
+            for a in range(PAIR):
+                nc.tensor.matmul_mx(
+                    out=o_mx_ps[j][:, a, :],
+                    lhsT=z_codes[q][:, quad_columns(j, a)].bitcast(FP8X4),
+                    lhsT_scale=z_planes[q][:, quad_columns(j, a)],
+                    rhs=w_codes[:, GATE_O, :].bitcast(FP8X4),
+                    rhs_scale=w_planes[:, GATE_O * CH : (GATE_O + 1) * CH],
+                    start=True,
+                    stop=True,
+                )
+
+        def squash_gate(j, g):
+            if not exists(j):
+                return
+            gates[j, g] = work.tile([P, PAIR, CH], F32, tag="gate%d" % g, name="gate%d" % g)
+            nc.scalar.activation(out=gates[j, g][:], in_=gate_ps[j, g][:], func=gate_func[g])
+
+        def add_bias_o(j):
+            if not exists(j):
+                return
+            o_sum[j] = work.tile([P, PAIR, CH], F32, tag="o_sum", name="o_sum")
+            nc.vector.tensor_tensor(
+                out=o_sum[j][:],
+                in0=gate_ps[j, GATE_O][:],
+                in1=bias_o[:].unsqueeze(1).to_broadcast([P, PAIR, CH]),
+                op=ALU.add,
+            )
+
+        def add_mx_o(j):
+            if not exists(j):
+                return
+            nc.vector.tensor_tensor(out=o_sum[j][:], in0=o_mx_ps[j][:], in1=o_sum[j][:], op=ALU.add)
+
+        def squash_o(j):
+            if not exists(j):
+                return
+            gates[j, GATE_O] = work.tile([P, PAIR, CH], F32, tag="gate2", name="gate2")
+            nc.scalar.activation(out=gates[j, GATE_O][:], in_=o_sum[j][:], func=gate_func[GATE_O])
 
         def input_times_update(j):
+            if not exists(j):
+                return
             iu[j] = work.tile([P, PAIR, CH], F32, tag="iu", name="iu")
-            nc.vector.tensor_tensor(out=iu[j][:], in0=gates[GATES * j][:], in1=gates[GATES * j + 1][:], op=ALU.mult)
+            nc.vector.tensor_tensor(out=iu[j][:], in0=gates[j, GATE_I][:], in1=gates[j, GATE_U][:], op=ALU.mult)
 
         def cell(j):
-            res[j] = results.tile([P, PAIR, 2 * CH], F32, tag="res", name="res")
+            if not exists(j):
+                return
+            res[j] = work.tile([P, PAIR, 2 * CH], F32, tag="res", name="res")
             nc.vector.tensor_tensor(out=res[j][:, :, CH:], in0=iu[j][:], in1=pair_rows(fc_sb, j), op=ALU.add)
+            nc.sync.dma_start(out=out_view[:, j * PAIR : (j + 1) * PAIR, CH:], in_=res[j][:, :, CH:])
 
         def squash_cell(j):
+            if not exists(j):
+                return
             tanh_c[j] = work.tile([P, PAIR, CH], F32, tag="tanh_c", name="tanh_c")
             nc.scalar.activation(out=tanh_c[j][:], in_=res[j][:, :, CH:], func=ACT.Tanh)
 
         def hidden(j):
-            nc.vector.tensor_tensor(out=res[j][:, :, :CH], in0=gates[GATES * j + 2][:], in1=tanh_c[j][:], op=ALU.mult)
-            nc.sync.dma_start(out=out_view[:, j * PAIR : (j + 1) * PAIR, :], in_=res[j][:])
+            if not exists(j):
+                return
+            nc.vector.tensor_tensor(out=res[j][:, :, :CH], in0=gates[j, GATE_O][:], in1=tanh_c[j][:], op=ALU.mult)
+            nc.sync.dma_start(out=out_view[:, j * PAIR : (j + 1) * PAIR, :CH], in_=res[j][:, :, :CH])
 
-        with tc.manual_schedule():
-            for j in range(QUAD // PAIR):
-                transpose_z(j)
-                copy_z(j)
-            for j in range(QUAD // PAIR):
-                quantise(j)
-                transpose_h(j)
-                copy_h(j)
+        bias_cols = consts.tile([P, BLOCKS], F32)
+        uT = consts.tile([P, HALVES, GATES * CH], BF16)
 
-            bias_ps = psum_gate.tile([P, P], BF16, tag="gate_ps")
+        def transpose_bias():
+            bias_ps = psum_one.tile([P, P], BF16, tag="hT_ps")
             nc.tensor.transpose(bias_ps[:], bias_rows[:], ident_bf16[:])
-            bias_cols = consts.tile([P, BLOCKS], F32)
             nc.vector.tensor_copy(out=bias_cols[:], in_=bias_ps[:, :BLOCKS])
 
-            uT = consts.tile([P, HALVES, GATES * CH], BF16)
-            for g in range(GATES):
-                uT_ps = psum_gate.tile([P, HALVES, HALVES, P], BF16, tag="gate_ps")
+        def transpose_hidden_weights():
+            for g, tag in enumerate(("o_plain_ps", "o_mx_ps", "hT_ps")):
+                uT_ps = psum_one.tile([P, HALVES, HALVES, P], BF16, tag=tag)
                 for kc in range(HALVES):
                     for half in range(HALVES):
                         nc.tensor.transpose(
@@ -289,37 +353,46 @@ def tile_treelstm_pb_t_kernel(
                     out=uT[:, :, g * CH : (g + 1) * CH], in_=uT_ps[:].rearrange("p kc half n -> p kc (half n)")
                 )
 
-            for j in range(-(QUAD // PAIR), PAIRS):
-                next_quad = (j * PAIR + QUAD) // QUAD
-                if j + AHEAD < PAIRS:
-                    transpose_z(j + AHEAD)
-                    transpose_h(j + AHEAD)
-                    copy_z(j + AHEAD)
-                    copy_h(j + AHEAD)
-                if j > 0:
-                    cell(j - 1)
-                    squash_cell(j - 1)
-                if j >= 0:
-                    for g in range(GATES):
-                        for i in range(PIECES):
-                            bring_in(j * GATES + g, i)
-                for g in range(GATES):
-                    s = j * GATES + g
-                    for i in range(PIECES):
-                        if i == PIECES - 1 and next_quad < QUADS:
-                            mx_block(next_quad, s % BLOCKS)
-                        if j >= 0:
-                            add_hidden(s, i)
-                    if j >= 0:
-                        squash_gate(s)
-                    if next_quad < QUADS:
-                        block_out(next_quad, s % BLOCKS)
-                    if g == 0 and j > 0:
-                        hidden(j - 1)
-                    if g == 1 and j >= 0:
-                        input_times_update(j)
-                    if g == 2 and j + AHEAD < PAIRS:
-                        quantise(j + AHEAD)
-            cell(PAIRS - 1)
-            squash_cell(PAIRS - 1)
-            hidden(PAIRS - 1)
+        def one_round(j):
+            hidden(j - 2)
+            squash_o(j - 1)
+            input_times_update(j - 1)
+
+            next_quad = (j * PAIR + QUAD) // QUAD
+            run = [j % (QUAD // PAIR) * HALVES + r for r in range(HALVES)] if 0 <= next_quad < QUADS else []
+            for i in range(PIECES):
+                add_hidden(j, GATE_I, i)
+                if i == 0:
+                    for b in run:
+                        mx_block(next_quad, b)
+                    transpose_h(j + H_AHEAD)
+                transpose_z(j + Z_AHEAD, i)
+            squash_gate(j, GATE_I)
+            for b in run:
+                block_out(next_quad, b)
+            copy_h(j + H_AHEAD)
+            copy_z(j + Z_AHEAD)
+            cell(j - 1)
+            squash_cell(j - 1)
+
+            for i in range(PIECES):
+                add_hidden(j, GATE_O, i)
+                if i == PIECES - 1:
+                    mx_o(j)
+                bring_in(j, GATE_U, i)
+            add_bias_o(j)
+            quantise(j + Z_AHEAD - 1)
+
+            for i in range(PIECES):
+                add_hidden(j, GATE_U, i)
+                bring_in(j + 1, GATE_I, i)
+            add_mx_o(j)
+            squash_gate(j, GATE_U)
+
+        with tc.manual_schedule():
+            for j in range(-Z_AHEAD, PAIRS + 2):
+                if j == -(QUAD // PAIR):
+                    transpose_bias()
+                if j == -1:
+                    transpose_hidden_weights()
+                one_round(j)

@@ -116,7 +116,8 @@ def tile_treelstm_pb_t_kernel(
                 in_=gate_words[g].rearrange("o p n t -> (o p) (n t)").bitcast(I32),
             )
 
-        load(z_sb, z_view, 0)
+        for first in range(0, QUAD, PAIR):
+            nc.sync.dma_start(out=z_sb[0][:, first : first + PAIR, :], in_=z_view[:, first : first + PAIR, :])
         load_weight(GATE_I)
         load_weight(GATE_U)
         load(z_sb, z_view, 1)
@@ -280,11 +281,20 @@ def tile_treelstm_pb_t_kernel(
                     stop=True,
                 )
 
+        def pair_rows_out(j):
+            return out_view[:, j * PAIR : (j + 1) * PAIR, :]
+
+        def parts(j):
+            if j == PAIRS - 1:
+                return [slice(a, a + 1) for a in range(PAIR)]
+            return [slice(0, PAIR)]
+
         def squash_gate(j, g):
             if not exists(j):
                 return
             gates[j, g] = work.tile([P, PAIR, CH], F32, tag="gate%d" % g, name="gate%d" % g)
-            nc.scalar.activation(out=gates[j, g][:], in_=gate_ps[j, g][:], func=gate_func[g])
+            for part in parts(j) if g == GATE_U else [slice(0, PAIR)]:
+                nc.scalar.activation(out=gates[j, g][:, part, :], in_=gate_ps[j, g][:, part, :], func=gate_func[g])
 
         def add_bias_o(j):
             if not exists(j):
@@ -312,26 +322,36 @@ def tile_treelstm_pb_t_kernel(
             if not exists(j):
                 return
             iu[j] = work.tile([P, PAIR, CH], F32, tag="iu", name="iu")
-            nc.vector.tensor_tensor(out=iu[j][:], in0=gates[j, GATE_I][:], in1=gates[j, GATE_U][:], op=ALU.mult)
+            for part in parts(j):
+                nc.vector.tensor_tensor(
+                    out=iu[j][:, part, :], in0=gates[j, GATE_I][:, part, :], in1=gates[j, GATE_U][:, part, :], op=ALU.mult
+                )
 
         def cell(j):
             if not exists(j):
                 return
             res[j] = work.tile([P, PAIR, 2 * CH], F32, tag="res", name="res")
-            nc.vector.tensor_tensor(out=res[j][:, :, CH:], in0=iu[j][:], in1=pair_rows(fc_sb, j), op=ALU.add)
-            nc.sync.dma_start(out=out_view[:, j * PAIR : (j + 1) * PAIR, CH:], in_=res[j][:, :, CH:])
+            for part in parts(j):
+                nc.vector.tensor_tensor(
+                    out=res[j][:, part, CH:], in0=iu[j][:, part, :], in1=pair_rows(fc_sb, j)[:, part, :], op=ALU.add
+                )
+                nc.sync.dma_start(out=pair_rows_out(j)[:, part, CH:], in_=res[j][:, part, CH:])
 
         def squash_cell(j):
             if not exists(j):
                 return
             tanh_c[j] = work.tile([P, PAIR, CH], F32, tag="tanh_c", name="tanh_c")
-            nc.scalar.activation(out=tanh_c[j][:], in_=res[j][:, :, CH:], func=ACT.Tanh)
+            for part in parts(j):
+                nc.scalar.activation(out=tanh_c[j][:, part, :], in_=res[j][:, part, CH:], func=ACT.Tanh)
 
         def hidden(j):
             if not exists(j):
                 return
-            nc.vector.tensor_tensor(out=res[j][:, :, :CH], in0=gates[j, GATE_O][:], in1=tanh_c[j][:], op=ALU.mult)
-            nc.sync.dma_start(out=out_view[:, j * PAIR : (j + 1) * PAIR, :CH], in_=res[j][:, :, :CH])
+            for part in parts(j):
+                nc.vector.tensor_tensor(
+                    out=res[j][:, part, :CH], in0=gates[j, GATE_O][:, part, :], in1=tanh_c[j][:, part, :], op=ALU.mult
+                )
+                nc.sync.dma_start(out=pair_rows_out(j)[:, part, :CH], in_=res[j][:, part, :CH])
 
         bias_cols = consts.tile([P, BLOCKS], F32)
         uT = consts.tile([P, HALVES, GATES * CH], BF16)
@@ -365,8 +385,11 @@ def tile_treelstm_pb_t_kernel(
                 if i == 0:
                     for b in run:
                         mx_block(next_quad, b)
+                if i == 1:
                     transpose_h(j + H_AHEAD)
-                transpose_z(j + Z_AHEAD, i)
+                    transpose_z(j + Z_AHEAD, 0)
+                if i >= 1:
+                    transpose_z(j + Z_AHEAD, i)
             squash_gate(j, GATE_I)
             for b in run:
                 block_out(next_quad, b)
@@ -377,9 +400,12 @@ def tile_treelstm_pb_t_kernel(
 
             for i in range(PIECES):
                 add_hidden(j, GATE_O, i)
-                if i == PIECES - 1:
+                if i == PIECES - 2:
                     mx_o(j)
-                bring_in(j, GATE_U, i)
+                if i == PIECES - 1:
+                    bring_in(j, GATE_U, PIECES - 2)
+                if i != PIECES - 2:
+                    bring_in(j, GATE_U, i)
             add_bias_o(j)
             quantise(j + Z_AHEAD - 1)
 

@@ -95,12 +95,10 @@ def tile_treelstm_pb_t_kernel(
             if q < QUADS:
                 nc.sync.dma_start(out=tiles_sb[q][:], in_=view[:, q * QUAD : (q + 1) * QUAD, :])
 
-        for g, bias in ((GATE_I, b_i), (GATE_U, b_u)):
-            nc.scalar.dma_start(
+        def load_bias(g, bias):
+            nc.sync.dma_start(
                 out=bias_rows[HALVES * g : HALVES * (g + 1), :], in_=bias.rearrange("(half c) -> half c", c=P)
             )
-        bias_o = consts.tile([P, CH], BF16)
-        nc.scalar.dma_start(out=bias_o[:], in_=b_o.partition_broadcast(P))
 
         w_codes = consts.tile([P, GATES, 4 * CH], U8, align_bytes=64)
 
@@ -116,20 +114,47 @@ def tile_treelstm_pb_t_kernel(
                 in_=gate_words[g].rearrange("o p n t -> (o p) (n t)").bitcast(I32),
             )
 
-        for first in range(0, QUAD, PAIR):
-            nc.sync.dma_start(out=z_sb[0][:, first : first + PAIR, :], in_=z_view[:, first : first + PAIR, :])
-        load_weight(GATE_I)
-        load_weight(GATE_U)
-        load(z_sb, z_view, 1)
-        load(h_sb, h_view, 0)
         u_rows = consts.tile([P, GATES, HALVES, CH], BF16)
-        for g in range(GATES):
+
+        def load_u(g):
             nc.sync.dma_start(
                 out=u_rows[:, g, :, :], in_=gate_hidden_weight[g].rearrange("(half p) k -> p half k", p=P)
             )
-        load_weight(GATE_O)
+
+        def load_scales(g, quadrants):
+            rows = gate_scales[g].rearrange("o q n -> (o q) n")
+            for quadrant in quadrants:
+                nc.sync.dma_start(
+                    out=w_planes[32 * quadrant : 32 * quadrant + 4, g * CH : (g + 1) * CH].bitcast(I32),
+                    in_=rows[4 * quadrant : 4 * quadrant + 4, :].bitcast(I32),
+                )
+
+        def load_codes(g):
+            nc.sync.dma_start(
+                out=w_codes[:, g, :].bitcast(I32),
+                in_=gate_words[g].rearrange("o p n t -> (o p) (n t)").bitcast(I32),
+            )
+
+        def load_on(queue, tiles_sb, view, q):
+            queue.dma_start(out=tiles_sb[q][:], in_=view[:, q * QUAD : (q + 1) * QUAD, :])
+        for first in range(0, QUAD, PAIR):
+            nc.sync.dma_start(out=z_sb[0][:, first : first + PAIR, :], in_=z_view[:, first : first + PAIR, :])
+        load(z_sb, z_view, 1)
+        load_bias(GATE_I, b_i)
+        load_bias(GATE_U, b_u)
+        load_bias(GATE_O, b_o)
+        load_scales(GATE_I, range(4))
+        load_codes(GATE_I)
+        load(h_sb, h_view, 0)
+        load_u(0)
+        load_u(1)
+        load_u(2)
+        load_scales(GATE_U, range(4))
+        load_codes(GATE_U)
         load(z_sb, z_view, 2)
         load(h_sb, h_view, 1)
+        load_codes(GATE_O)
+        load_scales(GATE_O, range(4))
         for q in range(QUADS):
             load(fc_sb, fc_view, q)
             load(z_sb, z_view, q + 3)
@@ -354,12 +379,25 @@ def tile_treelstm_pb_t_kernel(
                 nc.sync.dma_start(out=pair_rows_out(j)[:, part, :CH], in_=res[j][:, part, :CH])
 
         bias_cols = consts.tile([P, BLOCKS], F32)
+        bias_cols_o = consts.tile([P, HALVES], BF16)
+        bias_o = consts.tile([P, CH], F32)
         uT = consts.tile([P, HALVES, GATES * CH], BF16)
 
         def transpose_bias():
             bias_ps = psum_one.tile([P, P], BF16, tag="hT_ps")
             nc.tensor.transpose(bias_ps[:], bias_rows[:], ident_bf16[:])
             nc.vector.tensor_copy(out=bias_cols[:], in_=bias_ps[:, :BLOCKS])
+            nc.vector.tensor_copy(out=bias_cols_o[:], in_=bias_ps[:, HALVES * GATE_O : HALVES * (GATE_O + 1)])
+            spread_ps = psum_one.tile([P, CH], F32, tag="o_mx_ps", name="spread_ps")
+            for half in range(HALVES):
+                nc.tensor.matmul(
+                    spread_ps[:, half * P : (half + 1) * P],
+                    lhsT=bias_cols_o[:, half : half + 1].to_broadcast([P, P]),
+                    rhs=ident_bf16[:],
+                    start=True,
+                    stop=True,
+                )
+            nc.vector.tensor_copy(out=bias_o[:], in_=spread_ps[:])
 
         def transpose_hidden_weights():
             for g, tag in enumerate(("o_plain_ps", "o_mx_ps", "hT_ps")):

@@ -218,15 +218,15 @@ def tile_treelstm_pb_t_kernel(
                 out=z_codes[q][:, nodes].bitcast(FP8X4), scales=z_planes[q][:, nodes], in_=grouped[j][:]
             )
 
-        def transpose_h(j):
+        def transpose_h(j, i):
             if not exists(j):
                 return
-            hT_ps[j] = psum_one.tile([P, PAIR, HALVES, P], BF16, tag="hT_ps", name="hT_ps")
-            for a in range(PAIR):
-                for kc in range(HALVES):
-                    nc.tensor.transpose(
-                        hT_ps[j][:, a, kc, :], pair_rows(h_sb, j)[:, a, kc * P : (kc + 1) * P], ident_bf16[:]
-                    )
+            a, kc = divmod(i, HALVES)
+            if i == 0:
+                hT_ps[j] = psum_one.tile([P, PAIR, HALVES, P], BF16, tag="hT_ps", name="hT_ps")
+            nc.tensor.transpose(
+                hT_ps[j][:, a, kc, :], pair_rows(h_sb, j)[:, a, kc * P : (kc + 1) * P], ident_bf16[:]
+            )
 
         def copy_h(j):
             if not exists(j):
@@ -423,11 +423,12 @@ def tile_treelstm_pb_t_kernel(
                 if i == 0:
                     for b in run:
                         mx_block(next_quad, b)
-                if i == 1:
-                    transpose_h(j + H_AHEAD)
-                    transpose_z(j + Z_AHEAD, 0)
-                if i >= 1:
-                    transpose_z(j + Z_AHEAD, i)
+                else:
+                    transpose_z(j + Z_AHEAD, i - 1)
+                    transpose_h(j + H_AHEAD, i - 1)
+            transpose_h(j + H_AHEAD, PIECES - 1)
+            add_hidden(j, GATE_O, 0)
+            transpose_z(j + Z_AHEAD, PIECES - 1)
             squash_gate(j, GATE_I)
             for b in run:
                 block_out(next_quad, b)
@@ -436,13 +437,12 @@ def tile_treelstm_pb_t_kernel(
             cell(j - 1)
             squash_cell(j - 1)
 
-            for i in range(PIECES):
+            for i in range(1, PIECES):
                 add_hidden(j, GATE_O, i)
                 if i == PIECES - 2:
                     mx_o(j)
-                if i == PIECES - 1:
-                    bring_in(j, GATE_U, PIECES - 2)
-                if i != PIECES - 2:
+                else:
+                    bring_in(j, GATE_U, i - 1)
                     bring_in(j, GATE_U, i)
             add_bias_o(j)
             quantise(j + Z_AHEAD - 1)

@@ -75,8 +75,7 @@ def tile_treelstm_pb_t_kernel(
 
         w_planes = consts.tile([P, GATES * CH], U8, align_bytes=64)
         nc.vector.memset(w_planes[:].bitcast(I32), 0)
-        bias_rows = consts.tile([P, P], BF16)
-        nc.vector.memset(bias_rows[:], 0.0)
+        bias_cols = [consts.tile([P, HALVES], BF16, name="bias_cols%d" % g) for g in range(GATES)]
 
         ident_f32 = consts.tile([P, P], F32)
         make_identity(nc, ident_f32[:])
@@ -95,10 +94,8 @@ def tile_treelstm_pb_t_kernel(
             if q < QUADS:
                 nc.sync.dma_start(out=tiles_sb[q][:], in_=view[:, q * QUAD : (q + 1) * QUAD, :])
 
-        def load_bias(g, bias):
-            nc.sync.dma_start(
-                out=bias_rows[HALVES * g : HALVES * (g + 1), :], in_=bias.rearrange("(half c) -> half c", c=P)
-            )
+        def load_bias(queue, g, bias):
+            queue.dma_start(out=bias_cols[g][:], in_=bias.rearrange("(half p) -> p half", p=P))
 
         w_codes = consts.tile([P, GATES, 4 * CH], U8, align_bytes=64)
 
@@ -137,21 +134,21 @@ def tile_treelstm_pb_t_kernel(
 
         def load_on(queue, tiles_sb, view, q):
             queue.dma_start(out=tiles_sb[q][:], in_=view[:, q * QUAD : (q + 1) * QUAD, :])
-        for first in range(0, QUAD, PAIR):
-            nc.sync.dma_start(out=z_sb[0][:, first : first + PAIR, :], in_=z_view[:, first : first + PAIR, :])
-        load(z_sb, z_view, 1)
-        load_bias(GATE_I, b_i)
-        load_bias(GATE_U, b_u)
-        load_bias(GATE_O, b_o)
+        load_bias(nc.gpsimd, GATE_I, b_i)
+        load_bias(nc.gpsimd, GATE_U, b_u)
+        nc.sync.dma_start(out=z_sb[0][:, 0:2, :], in_=z_view[:, 0:2, :])
+        nc.sync.dma_start(out=z_sb[0][:, 2:4, :], in_=z_view[:, 2:4, :])
         load_scales(GATE_I, range(4))
         load_codes(GATE_I)
+        load(z_sb, z_view, 1)
         load(h_sb, h_view, 0)
-        load_u(0)
-        load_u(1)
-        load_u(2)
+        load_u(GATE_I)
+        load_bias(nc.sync, GATE_O, b_o)
         load_scales(GATE_U, range(4))
         load_codes(GATE_U)
         load(z_sb, z_view, 2)
+        load_u(GATE_O)
+        load_u(GATE_U)
         load(h_sb, h_view, 1)
         load_codes(GATE_O)
         load_scales(GATE_O, range(4))
@@ -252,13 +249,13 @@ def tile_treelstm_pb_t_kernel(
                 nc.vector.tensor_scalar(
                     out=block_sb[q, b][:],
                     in0=block_ps[q, b][:],
-                    scalar1=bias_cols[:, b : b + 1],
+                    scalar1=bias_cols[b // HALVES][:, b % HALVES : b % HALVES + 1],
                     scalar2=None,
                     op0=ALU.add,
                 )
             else:
                 nc.scalar.activation(
-                    out=block_sb[q, b][:], in_=block_ps[q, b][:], func=ACT.Identity, bias=bias_cols[:, b : b + 1]
+                    out=block_sb[q, b][:], in_=block_ps[q, b][:], func=ACT.Identity, bias=bias_cols[b // HALVES][:, b % HALVES : b % HALVES + 1]
                 )
 
         def bring_in(j, g, i):
@@ -378,38 +375,31 @@ def tile_treelstm_pb_t_kernel(
                 )
                 nc.sync.dma_start(out=pair_rows_out(j)[:, part, :CH], in_=res[j][:, part, :CH])
 
-        bias_cols = consts.tile([P, BLOCKS], F32)
-        bias_cols_o = consts.tile([P, HALVES], BF16)
         bias_o = consts.tile([P, CH], F32)
         uT = consts.tile([P, HALVES, GATES * CH], BF16)
 
-        def transpose_bias():
-            bias_ps = psum_one.tile([P, P], BF16, tag="hT_ps")
-            nc.tensor.transpose(bias_ps[:], bias_rows[:], ident_bf16[:])
-            nc.vector.tensor_copy(out=bias_cols[:], in_=bias_ps[:, :BLOCKS])
-            nc.vector.tensor_copy(out=bias_cols_o[:], in_=bias_ps[:, HALVES * GATE_O : HALVES * (GATE_O + 1)])
+        def spread_bias_o():
             spread_ps = psum_one.tile([P, CH], F32, tag="o_mx_ps", name="spread_ps")
             for half in range(HALVES):
                 nc.tensor.matmul(
                     spread_ps[:, half * P : (half + 1) * P],
-                    lhsT=bias_cols_o[:, half : half + 1].to_broadcast([P, P]),
+                    lhsT=bias_cols[GATE_O][:, half : half + 1].to_broadcast([P, P]),
                     rhs=ident_bf16[:],
                     start=True,
                     stop=True,
                 )
             nc.vector.tensor_copy(out=bias_o[:], in_=spread_ps[:])
 
-        def transpose_hidden_weights():
-            for g, tag in enumerate(("o_plain_ps", "o_mx_ps", "hT_ps")):
-                uT_ps = psum_one.tile([P, HALVES, HALVES, P], BF16, tag=tag)
-                for kc in range(HALVES):
-                    for half in range(HALVES):
-                        nc.tensor.transpose(
-                            uT_ps[:, kc, half, :], u_rows[:, g, half, kc * P : (kc + 1) * P], ident_bf16[:]
-                        )
-                nc.vector.tensor_copy(
-                    out=uT[:, :, g * CH : (g + 1) * CH], in_=uT_ps[:].rearrange("p kc half n -> p kc (half n)")
-                )
+        def transpose_hidden_weight(g, tag):
+            uT_ps = psum_one.tile([P, HALVES, HALVES, P], BF16, tag=tag, name="uT_ps")
+            for kc in range(HALVES):
+                for half in range(HALVES):
+                    nc.tensor.transpose(
+                        uT_ps[:, kc, half, :], u_rows[:, g, half, kc * P : (kc + 1) * P], ident_bf16[:]
+                    )
+            nc.vector.tensor_copy(
+                out=uT[:, :, g * CH : (g + 1) * CH], in_=uT_ps[:].rearrange("p kc half n -> p kc (half n)")
+            )
 
         def one_round(j):
             hidden(j - 2)
@@ -455,8 +445,11 @@ def tile_treelstm_pb_t_kernel(
 
         with tc.manual_schedule():
             for j in range(-Z_AHEAD, PAIRS + 2):
-                if j == -(QUAD // PAIR):
-                    transpose_bias()
                 if j == -1:
-                    transpose_hidden_weights()
+                    spread_bias_o()
                 one_round(j)
+                if j == -2:
+                    transpose_hidden_weight(GATE_I, "o_plain_ps")
+                if j == -1:
+                    transpose_hidden_weight(GATE_O, "o_plain_ps")
+                    transpose_hidden_weight(GATE_U, "o_mx_ps")

@@ -402,10 +402,6 @@ def tile_treelstm_pb_t_kernel(
             )
 
         def one_round(j):
-            hidden(j - 2)
-            squash_o(j - 1)
-            input_times_update(j - 1)
-
             next_quad = (j * PAIR + QUAD) // QUAD
             run = [j % (QUAD // PAIR) * HALVES + r for r in range(HALVES)] if 0 <= next_quad < QUADS else []
             for i in range(PIECES):
@@ -422,10 +418,12 @@ def tile_treelstm_pb_t_kernel(
             squash_gate(j, GATE_I)
             for b in run:
                 block_out(next_quad, b)
+            quantise(j + Z_AHEAD - 1)
             copy_h(j + H_AHEAD)
             copy_z(j + Z_AHEAD)
-            cell(j - 1)
-            squash_cell(j - 1)
+            input_times_update(j - 1)
+            hidden(j - 2)
+            squash_o(j - 1)
 
             for i in range(1, PIECES):
                 add_hidden(j, GATE_O, i)
@@ -435,13 +433,14 @@ def tile_treelstm_pb_t_kernel(
                     bring_in(j, GATE_U, i - 1)
                     bring_in(j, GATE_U, i)
             add_bias_o(j)
-            quantise(j + Z_AHEAD - 1)
+            cell(j - 1)
 
             for i in range(PIECES):
                 add_hidden(j, GATE_U, i)
                 bring_in(j + 1, GATE_I, i)
             add_mx_o(j)
             squash_gate(j, GATE_U)
+            squash_cell(j - 1)
 
         with tc.manual_schedule():
             for j in range(-Z_AHEAD, PAIRS + 2):

@@ -134,28 +134,36 @@ def tile_treelstm_pb_t_kernel(
 
         def load_on(queue, tiles_sb, view, q):
             queue.dma_start(out=tiles_sb[q][:], in_=view[:, q * QUAD : (q + 1) * QUAD, :])
+        def load_pair(j):
+            first = j * PAIR % QUAD
+            nc.sync.dma_start(
+                out=z_sb[j * PAIR // QUAD][:, first : first + PAIR, :], in_=z_view[:, j * PAIR : (j + 1) * PAIR, :]
+            )
+
         load_bias(nc.gpsimd, GATE_I, b_i)
         load_bias(nc.gpsimd, GATE_U, b_u)
-        nc.sync.dma_start(out=z_sb[0][:, 0:2, :], in_=z_view[:, 0:2, :])
-        nc.sync.dma_start(out=z_sb[0][:, 2:4, :], in_=z_view[:, 2:4, :])
-        load_scales(GATE_I, range(4))
+        load_pair(0)
+        load_pair(1)
         load_codes(GATE_I)
+        load_scales(GATE_I, range(4))
         load(z_sb, z_view, 1)
+        load_bias(nc.sync, GATE_O, b_o)
         load(h_sb, h_view, 0)
         load_u(GATE_I)
-        load_bias(nc.sync, GATE_O, b_o)
         load_scales(GATE_U, range(4))
         load_codes(GATE_U)
-        load(z_sb, z_view, 2)
-        load_u(GATE_O)
+        load_pair(4)
         load_u(GATE_U)
+        load_u(GATE_O)
         load(h_sb, h_view, 1)
         load_codes(GATE_O)
+        load_pair(5)
         load_scales(GATE_O, range(4))
+        load(z_sb, z_view, 3)
         for q in range(QUADS):
             load(fc_sb, fc_view, q)
-            load(z_sb, z_view, q + 3)
             load(h_sb, h_view, q + 2)
+            load(z_sb, z_view, q + 4)
 
         zT_ps = {}
         hT_ps = {}
@@ -291,7 +299,10 @@ def tile_treelstm_pb_t_kernel(
             if not exists(j):
                 return
             q = j * PAIR // QUAD
-            o_mx_ps[j] = psum_one.tile([P, PAIR, CH], F32, tag="o_mx_ps", name="o_mx_ps")
+            if j == PAIRS - 1:
+                o_mx_ps[j] = psum_two.tile([P, PAIR, CH], F32, tag="block_ps", name="last_o_mx_ps")
+            else:
+                o_mx_ps[j] = psum_one.tile([P, PAIR, CH], F32, tag="o_mx_ps", name="o_mx_ps")
             for a in range(PAIR):
                 nc.tensor.matmul_mx(
                     out=o_mx_ps[j][:, a, :],
@@ -318,21 +329,21 @@ def tile_treelstm_pb_t_kernel(
             for part in parts(j) if g == GATE_U else [slice(0, PAIR)]:
                 nc.scalar.activation(out=gates[j, g][:, part, :], in_=gate_ps[j, g][:, part, :], func=gate_func[g])
 
-        def add_bias_o(j):
+        def add_bias_o(j, first):
             if not exists(j):
                 return
             o_sum[j] = work.tile([P, PAIR, CH], F32, tag="o_sum", name="o_sum")
             nc.vector.tensor_tensor(
                 out=o_sum[j][:],
-                in0=gate_ps[j, GATE_O][:],
+                in0=first[:],
                 in1=bias_o[:].unsqueeze(1).to_broadcast([P, PAIR, CH]),
                 op=ALU.add,
             )
 
-        def add_mx_o(j):
+        def join_o(j, second):
             if not exists(j):
                 return
-            nc.vector.tensor_tensor(out=o_sum[j][:], in0=o_mx_ps[j][:], in1=o_sum[j][:], op=ALU.add)
+            nc.vector.tensor_tensor(out=o_sum[j][:], in0=second[:], in1=o_sum[j][:], op=ALU.add)
 
         def squash_o(j):
             if not exists(j):
@@ -409,6 +420,8 @@ def tile_treelstm_pb_t_kernel(
                 if i == 0:
                     for b in run:
                         mx_block(next_quad, b)
+                    if j == PAIRS - 2:
+                        mx_o(j + 1)
                 else:
                     transpose_z(j + Z_AHEAD, i - 1)
                     transpose_h(j + H_AHEAD, i - 1)
@@ -418,28 +431,39 @@ def tile_treelstm_pb_t_kernel(
             squash_gate(j, GATE_I)
             for b in run:
                 block_out(next_quad, b)
+            if j == PAIRS - 2:
+                add_bias_o(j + 1, o_mx_ps[j + 1])
             quantise(j + Z_AHEAD - 1)
             copy_h(j + H_AHEAD)
             copy_z(j + Z_AHEAD)
             input_times_update(j - 1)
-            hidden(j - 2)
+            if j != PAIRS:
+                hidden(j - 2)
             squash_o(j - 1)
 
             for i in range(1, PIECES):
                 add_hidden(j, GATE_O, i)
-                if i == PIECES - 2:
-                    mx_o(j)
-                else:
+                if i != PIECES - 2:
                     bring_in(j, GATE_U, i - 1)
                     bring_in(j, GATE_U, i)
-            add_bias_o(j)
+            if exists(j) and j != PAIRS - 1:
+                add_bias_o(j, gate_ps[j, GATE_O])
             cell(j - 1)
 
             for i in range(PIECES):
                 add_hidden(j, GATE_U, i)
+                if i == 0:
+                    if j != PAIRS - 1:
+                        mx_o(j)
+                    continue
+                if i == 1:
+                    bring_in(j + 1, GATE_I, 0)
                 bring_in(j + 1, GATE_I, i)
-            add_mx_o(j)
+            if exists(j):
+                join_o(j, gate_ps[j, GATE_O] if j == PAIRS - 1 else o_mx_ps[j])
             squash_gate(j, GATE_U)
+            if j == PAIRS:
+                hidden(j - 2)
             squash_cell(j - 1)
 
         with tc.manual_schedule():

from contextlib import ExitStack

import concourse.mybir as mybir
from concourse.masks import make_identity

F32 = mybir.dt.float32
BF16 = mybir.dt.bfloat16
I32 = mybir.dt.int32
U32 = mybir.dt.uint32
U8 = mybir.dt.uint8
FP8X4 = mybir.dt.float8_e4m3fn_x4
ACT = mybir.ActivationFunctionType
ALU = mybir.AluOpType

P = 128
NODES = 4096
FEAT = 512
CH = 256
HALVES = CH // P
TILES = NODES // P
PAIR = 2
PAIRS = TILES // PAIR
QUAD = 4
QUADS = TILES // QUAD
GATES = 3
GATE_I = 0
GATE_U = 1
GATE_O = 2
BLOCKS = 2 * HALVES
PIECES = PAIR * HALVES
Z_AHEAD = 5
H_AHEAD = 2

FLOPS = 2 * NODES * GATES * CH * (FEAT + CH)


def tile_treelstm_pb_t_kernel(
    tc,
    z0,
    h_tilde,
    fc_sum,
    W_i_words,
    W_i_scales,
    U_i,
    b_i,
    W_o_words,
    W_o_scales,
    U_o,
    b_o,
    W_u_words,
    W_u_scales,
    U_u,
    b_u,
    out,
):
    nc = tc.nc
    gate_words = [W_i_words, W_u_words, W_o_words]
    gate_scales = [W_i_scales, W_u_scales, W_o_scales]
    gate_hidden_weight = [U_i, U_u, U_o]
    gate_func = [ACT.Sigmoid, ACT.Tanh, ACT.Sigmoid]

    z_view = z0.rearrange("(p t) k -> p t k", t=TILES)
    h_view = h_tilde.rearrange("(p t) k -> p t k", t=TILES)
    fc_view = fc_sum.rearrange("(p t) c -> p t c", t=TILES)
    out_view = out.rearrange("(p t) c -> p t c", t=TILES)

    with ExitStack() as ctx:
        consts = ctx.enter_context(tc.tile_pool(name="consts", bufs=1))
        inputs = ctx.enter_context(tc.tile_pool(name="inputs", bufs=1))
        quads = ctx.enter_context(tc.tile_pool(name="quads", bufs=3))
        blocks = ctx.enter_context(tc.tile_pool(name="blocks", bufs=2))
        work = ctx.enter_context(tc.tile_pool(name="work", bufs=4))
        psum_one = ctx.enter_context(tc.psum_pool(name="psum_one", bufs=1))
        psum_two = ctx.enter_context(tc.psum_pool(name="psum_two", bufs=2))

        w_planes = consts.tile([P, GATES * CH], U8, align_bytes=64)
        nc.vector.memset(w_planes[:].bitcast(I32), 0)
        bias_cols = [consts.tile([P, HALVES], BF16, name="bias_cols%d" % g) for g in range(GATES)]

        ident_f32 = consts.tile([P, P], F32)
        make_identity(nc, ident_f32[:])
        ident_bf16 = consts.tile([P, P], BF16)
        make_identity(nc, ident_bf16[:])

        z_sb = []
        h_sb = []
        fc_sb = []
        for q in range(QUADS):
            z_sb.append(inputs.tile([P, QUAD, FEAT], BF16, name="z_sb%d" % q))
            h_sb.append(inputs.tile([P, QUAD, CH], BF16, name="h_sb%d" % q))
            fc_sb.append(inputs.tile([P, QUAD, CH], BF16, name="fc_sb%d" % q))

        def load(tiles_sb, view, q):
            if q < QUADS:
                nc.sync.dma_start(out=tiles_sb[q][:], in_=view[:, q * QUAD : (q + 1) * QUAD, :])

        def load_bias(queue, g, bias):
            queue.dma_start(out=bias_cols[g][:], in_=bias.rearrange("(half p) -> p half", p=P))

        w_codes = consts.tile([P, GATES, 4 * CH], U8, align_bytes=64)

        def load_weight(g):
            rows = gate_scales[g].rearrange("o q n -> (o q) n")
            for quadrant in range(4):
                nc.sync.dma_start(
                    out=w_planes[32 * quadrant : 32 * quadrant + 4, g * CH : (g + 1) * CH].bitcast(I32),
                    in_=rows[4 * quadrant : 4 * quadrant + 4, :].bitcast(I32),
                )
            nc.sync.dma_start(
                out=w_codes[:, g, :].bitcast(I32),
                in_=gate_words[g].rearrange("o p n t -> (o p) (n t)").bitcast(I32),
            )

        u_rows = consts.tile([P, GATES, HALVES, CH], BF16)

        def load_u(g):
            nc.sync.dma_start(
                out=u_rows[:, g, :, :], in_=gate_hidden_weight[g].rearrange("(half p) k -> p half k", p=P)
            )

        def load_scales(g, quadrants):
            rows = gate_scales[g].rearrange("o q n -> (o q) n")
            for quadrant in quadrants:
                nc.sync.dma_start(
                    out=w_planes[32 * quadrant : 32 * quadrant + 4, g * CH : (g + 1) * CH].bitcast(I32),
                    in_=rows[4 * quadrant : 4 * quadrant + 4, :].bitcast(I32),
                )

        def load_codes(g):
            nc.sync.dma_start(
                out=w_codes[:, g, :].bitcast(I32),
                in_=gate_words[g].rearrange("o p n t -> (o p) (n t)").bitcast(I32),
            )

        def load_on(queue, tiles_sb, view, q):
            queue.dma_start(out=tiles_sb[q][:], in_=view[:, q * QUAD : (q + 1) * QUAD, :])
        def load_pair(j):
            first = j * PAIR % QUAD
            nc.sync.dma_start(
                out=z_sb[j * PAIR // QUAD][:, first : first + PAIR, :], in_=z_view[:, j * PAIR : (j + 1) * PAIR, :]
            )

        load_bias(nc.gpsimd, GATE_I, b_i)
        load_bias(nc.gpsimd, GATE_U, b_u)
        load_pair(0)
        load_pair(1)
        load_codes(GATE_I)
        load_scales(GATE_I, range(4))
        load(z_sb, z_view, 1)
        load_bias(nc.sync, GATE_O, b_o)
        load(h_sb, h_view, 0)
        load_u(GATE_I)
        load_scales(GATE_U, range(4))
        load_codes(GATE_U)
        load_pair(4)
        load_u(GATE_U)
        load_u(GATE_O)
        load(h_sb, h_view, 1)
        load_codes(GATE_O)
        load_pair(5)
        load_scales(GATE_O, range(4))
        load(z_sb, z_view, 3)
        for q in range(QUADS):
            load(fc_sb, fc_view, q)
            load(h_sb, h_view, q + 2)
            load(z_sb, z_view, q + 4)

        zT_ps = {}
        hT_ps = {}
        grouped = {}
        hT = {}
        z_codes = {}
        z_planes = {}
        block_ps = {}
        block_sb = {}
        gate_ps = {}
        o_mx_ps = {}
        o_sum = {}
        gates = {}
        iu = {}
        res = {}
        tanh_c = {}

        def exists(j):
            return 0 <= j < PAIRS

        def pair_rows(tiles_sb, j):
            first = (j * PAIR) % QUAD
            return tiles_sb[(j * PAIR) // QUAD][:, first : first + PAIR, :]

        def quad_columns(j, a):
            return slice((j * PAIR % QUAD + a) * P, (j * PAIR % QUAD + a + 1) * P)

        def transpose_z(j, i):
            if not exists(j):
                return
            a, u = divmod(i, 2)
            if i == 0 and j < Z_AHEAD - 1:
                zT_ps[j] = psum_two.tile([P, PAIR, 2, P], F32, tag="gate_ps", name="zT_early_ps")
            elif i == 0:
                zT_ps[j] = psum_one.tile([P, PAIR, 2, P], F32, tag="zT_ps", name="zT_ps")
            words = pair_rows(z_sb, j)[:, a, :].bitcast(F32)
            nc.tensor.transpose(zT_ps[j][:, a, u, :], words[:, u : FEAT // 2 : 2], ident_f32[:])

        def copy_z(j):
            if not exists(j):
                return
            grouped[j] = work.tile([P, PAIR * P * 4], BF16, align_bytes=64, tag="grouped", name="grouped")
            nc.scalar.copy(
                out=grouped[j][:].bitcast(F32).rearrange("p (a n u) -> p a n u", a=PAIR, u=2),
                in_=zT_ps[j][:].rearrange("p a u n -> p a n u"),
            )

        def quantise(j):
            if not exists(j):
                return
            q = j * PAIR // QUAD
            if j * PAIR % QUAD == 0:
                z_codes[q] = quads.tile([P, QUAD * P], U32, align_bytes=64, tag="z_codes", name="z_codes")
                z_planes[q] = quads.tile([P, QUAD * P], U8, align_bytes=64, tag="z_planes", name="z_planes")
            nodes = slice(j * PAIR % QUAD * P, (j * PAIR % QUAD + PAIR) * P)
            nc.vector.quantize_mx(
                out=z_codes[q][:, nodes].bitcast(FP8X4), scales=z_planes[q][:, nodes], in_=grouped[j][:]
            )

        def transpose_h(j, i):
            if not exists(j):
                return
            a, kc = divmod(i, HALVES)
            if i == 0:
                hT_ps[j] = psum_one.tile([P, PAIR, HALVES, P], BF16, tag="hT_ps", name="hT_ps")
            nc.tensor.transpose(
                hT_ps[j][:, a, kc, :], pair_rows(h_sb, j)[:, a, kc * P : (kc + 1) * P], ident_bf16[:]
            )

        def copy_h(j):
            if not exists(j):
                return
            hT[j] = work.tile([P, PAIR, HALVES, P], BF16, tag="hT", name="hT")
            nc.scalar.copy(out=hT[j][:], in_=hT_ps[j][:])

        def mx_block(q, b):
            block_ps[q, b] = psum_two.tile([P, QUAD * P], F32, tag="block_ps", name="block_ps")
            nc.tensor.matmul_mx(
                out=block_ps[q, b][:],
                lhsT=w_codes[:, b // HALVES, (b % HALVES) * 4 * P : (b % HALVES + 1) * 4 * P].bitcast(FP8X4),
                lhsT_scale=w_planes[:, b * P : (b + 1) * P],
                rhs=z_codes[q][:].bitcast(FP8X4),
                rhs_scale=z_planes[q][:],
                start=True,
                stop=True,
            )

        def block_out(q, b):
            block_sb[q, b] = blocks.tile([P, QUAD * P], F32, tag="block_sb%d" % b, name="block_sb%d" % b)
            if b % 2 == 0:
                nc.vector.tensor_scalar(
                    out=block_sb[q, b][:],
                    in0=block_ps[q, b][:],
                    scalar1=bias_cols[b // HALVES][:, b % HALVES : b % HALVES + 1],
                    scalar2=None,
                    op0=ALU.add,
                )
            else:
                nc.scalar.activation(
                    out=block_sb[q, b][:], in_=block_ps[q, b][:], func=ACT.Identity, bias=bias_cols[b // HALVES][:, b % HALVES : b % HALVES + 1]
                )

        def bring_in(j, g, i):
            if not exists(j):
                return
            a, half = divmod(i, HALVES)
            if i == 0:
                gate_ps[j, g] = psum_two.tile([P, PAIR, CH], F32, tag="gate_ps", name="gate_ps")
            nc.tensor.matmul(
                gate_ps[j, g][:, a, half * P : (half + 1) * P],
                lhsT=block_sb[j * PAIR // QUAD, HALVES * g + half][:, quad_columns(j, a)],
                rhs=ident_f32[:],
                is_transpose=True,
                start=(i == 0),
                stop=False,
            )

        def add_hidden(j, g, i):
            if not exists(j):
                return
            a, kc = divmod(i, HALVES)
            if g == GATE_O and i == 0:
                gate_ps[j, g] = psum_one.tile([P, PAIR, CH], F32, tag="o_plain_ps", name="o_plain_ps")
            nc.tensor.matmul(
                gate_ps[j, g][:, a, :],
                lhsT=hT[j][:, a, kc, :],
                rhs=uT[:, kc, g * CH : (g + 1) * CH],
                start=(g == GATE_O and kc == 0),
                stop=(kc == HALVES - 1 if g == GATE_O else i == PIECES - 1),
            )

        def mx_o(j):
            if not exists(j):
                return
            q = j * PAIR // QUAD
            if j == PAIRS - 1:
                o_mx_ps[j] = psum_two.tile([P, PAIR, CH], F32, tag="block_ps", name="last_o_mx_ps")
            else:
                o_mx_ps[j] = psum_one.tile([P, PAIR, CH], F32, tag="o_mx_ps", name="o_mx_ps")
            for a in range(PAIR):
                nc.tensor.matmul_mx(
                    out=o_mx_ps[j][:, a, :],
                    lhsT=z_codes[q][:, quad_columns(j, a)].bitcast(FP8X4),
                    lhsT_scale=z_planes[q][:, quad_columns(j, a)],
                    rhs=w_codes[:, GATE_O, :].bitcast(FP8X4),
                    rhs_scale=w_planes[:, GATE_O * CH : (GATE_O + 1) * CH],
                    start=True,
                    stop=True,
                )

        def pair_rows_out(j):
            return out_view[:, j * PAIR : (j + 1) * PAIR, :]

        def parts(j):
            if j == PAIRS - 1:
                return [slice(a, a + 1) for a in range(PAIR)]
            return [slice(0, PAIR)]

        def squash_gate(j, g):
            if not exists(j):
                return
            gates[j, g] = work.tile([P, PAIR, CH], F32, tag="gate%d" % g, name="gate%d" % g)
            for part in parts(j) if g == GATE_U else [slice(0, PAIR)]:
                nc.scalar.activation(out=gates[j, g][:, part, :], in_=gate_ps[j, g][:, part, :], func=gate_func[g])

        def add_bias_o(j, first):
            if not exists(j):
                return
            o_sum[j] = work.tile([P, PAIR, CH], F32, tag="o_sum", name="o_sum")
            nc.vector.tensor_tensor(
                out=o_sum[j][:],
                in0=first[:],
                in1=bias_o[:].unsqueeze(1).to_broadcast([P, PAIR, CH]),
                op=ALU.add,
            )

        def join_o(j, second):
            if not exists(j):
                return
            nc.vector.tensor_tensor(out=o_sum[j][:], in0=second[:], in1=o_sum[j][:], op=ALU.add)

        def squash_o(j):
            if not exists(j):
                return
            gates[j, GATE_O] = work.tile([P, PAIR, CH], F32, tag="gate2", name="gate2")
            nc.scalar.activation(out=gates[j, GATE_O][:], in_=o_sum[j][:], func=gate_func[GATE_O])

        def input_times_update(j):
            if not exists(j):
                return
            iu[j] = work.tile([P, PAIR, CH], F32, tag="iu", name="iu")
            for part in parts(j):
                nc.vector.tensor_tensor(
                    out=iu[j][:, part, :], in0=gates[j, GATE_I][:, part, :], in1=gates[j, GATE_U][:, part, :], op=ALU.mult
                )

        def cell(j):
            if not exists(j):
                return
            res[j] = work.tile([P, PAIR, 2 * CH], F32, tag="res", name="res")
            for part in parts(j):
                nc.vector.tensor_tensor(
                    out=res[j][:, part, CH:], in0=iu[j][:, part, :], in1=pair_rows(fc_sb, j)[:, part, :], op=ALU.add
                )
                nc.sync.dma_start(out=pair_rows_out(j)[:, part, CH:], in_=res[j][:, part, CH:])

        def squash_cell(j):
            if not exists(j):
                return
            tanh_c[j] = work.tile([P, PAIR, CH], F32, tag="tanh_c", name="tanh_c")
            for part in parts(j):
                nc.scalar.activation(out=tanh_c[j][:, part, :], in_=res[j][:, part, CH:], func=ACT.Tanh)

        def hidden(j):
            if not exists(j):
                return
            for part in parts(j):
                nc.vector.tensor_tensor(
                    out=res[j][:, part, :CH], in0=gates[j, GATE_O][:, part, :], in1=tanh_c[j][:, part, :], op=ALU.mult
                )
                nc.sync.dma_start(out=pair_rows_out(j)[:, part, :CH], in_=res[j][:, part, :CH])

        bias_o = consts.tile([P, CH], F32)
        uT = consts.tile([P, HALVES, GATES * CH], BF16)

        def spread_bias_o():
            spread_ps = psum_one.tile([P, CH], F32, tag="o_mx_ps", name="spread_ps")
            for half in range(HALVES):
                nc.tensor.matmul(
                    spread_ps[:, half * P : (half + 1) * P],
                    lhsT=bias_cols[GATE_O][:, half : half + 1].to_broadcast([P, P]),
                    rhs=ident_bf16[:],
                    start=True,
                    stop=True,
                )
            nc.vector.tensor_copy(out=bias_o[:], in_=spread_ps[:])

        def transpose_hidden_weight(g, tag):
            uT_ps = psum_one.tile([P, HALVES, HALVES, P], BF16, tag=tag, name="uT_ps")
            for kc in range(HALVES):
                for half in range(HALVES):
                    nc.tensor.transpose(
                        uT_ps[:, kc, half, :], u_rows[:, g, half, kc * P : (kc + 1) * P], ident_bf16[:]
                    )
            nc.vector.tensor_copy(
                out=uT[:, :, g * CH : (g + 1) * CH], in_=uT_ps[:].rearrange("p kc half n -> p kc (half n)")
            )

        def one_round(j):
            next_quad = (j * PAIR + QUAD) // QUAD
            run = [j % (QUAD // PAIR) * HALVES + r for r in range(HALVES)] if 0 <= next_quad < QUADS else []
            for i in range(PIECES):
                add_hidden(j, GATE_I, i)
                if i == 0:
                    for b in run:
                        mx_block(next_quad, b)
                    if j == PAIRS - 2:
                        mx_o(j + 1)
                else:
                    transpose_z(j + Z_AHEAD, i - 1)
                    transpose_h(j + H_AHEAD, i - 1)
            transpose_h(j + H_AHEAD, PIECES - 1)
            add_hidden(j, GATE_O, 0)
            transpose_z(j + Z_AHEAD, PIECES - 1)
            squash_gate(j, GATE_I)
            for b in run:
                block_out(next_quad, b)
            if j == PAIRS - 2:
                add_bias_o(j + 1, o_mx_ps[j + 1])
            quantise(j + Z_AHEAD - 1)
            copy_h(j + H_AHEAD)
            copy_z(j + Z_AHEAD)
            input_times_update(j - 1)
            if j != PAIRS:
                hidden(j - 2)
            squash_o(j - 1)

            for i in range(1, PIECES):
                add_hidden(j, GATE_O, i)
                if i != PIECES - 2:
                    bring_in(j, GATE_U, i - 1)
                    bring_in(j, GATE_U, i)
            if exists(j) and j != PAIRS - 1:
                add_bias_o(j, gate_ps[j, GATE_O])
            cell(j - 1)

            for i in range(PIECES):
                add_hidden(j, GATE_U, i)
                if i == 0:
                    if j != PAIRS - 1:
                        mx_o(j)
                    continue
                if i == 1:
                    bring_in(j + 1, GATE_I, 0)
                bring_in(j + 1, GATE_I, i)
            if exists(j):
                join_o(j, gate_ps[j, GATE_O] if j == PAIRS - 1 else o_mx_ps[j])
            squash_gate(j, GATE_U)
            if j == PAIRS:
                hidden(j - 2)
            squash_cell(j - 1)

        with tc.manual_schedule():
            for j in range(-Z_AHEAD, PAIRS + 2):
                if j == -1:
                    spread_bias_o()
                one_round(j)
                if j == -2:
                    transpose_hidden_weight(GATE_I, "o_plain_ps")
                if j == -1:
                    transpose_hidden_weight(GATE_O, "o_plain_ps")
                    transpose_hidden_weight(GATE_U, "o_mx_ps")
